import numpy as np
import ml_dtypes


def mxq(x, axis, fmt="e4m3"):
    dtype, down = {"e4m3": (ml_dtypes.float8_e4m3fn, 7), "e5m2": (ml_dtypes.float8_e5m2, 14)}[fmt]
    v = np.moveaxis(np.asarray(x, np.float32).astype(ml_dtypes.bfloat16).astype(np.float64), axis, -1)
    blocks = v.reshape(v.shape[:-1] + (-1, 32))
    amax = np.abs(blocks).max(-1, keepdims=True)
    byte = np.maximum(np.where(amax > 0, np.frexp(amax)[1] - 1 + 127, 0) - down, 1)
    scale = np.exp2(byte - 127.0)
    codes = (blocks / scale).astype(np.float32).astype(dtype).astype(np.float64)
    return np.moveaxis((codes * scale).reshape(v.shape), -1, axis)


WIDE = False


def mx_kscale(k):
    if not WIDE:
        return np.ones(k)
    levels = np.array([18, -18])
    if k % 512:
        return np.exp2(np.random.permutation(np.resize(levels, k // 32))).repeat(32)
    a = np.empty((k // 512, 16))
    for p in range(k // 512):
        a[p, :8] = np.random.permutation(np.resize(levels, 8))
        for g in range(8):
            far = levels[np.abs(levels - a[p, g]) >= 10]
            a[p, g + 8] = far[np.random.randint(len(far))]
    return np.exp2(a.ravel()).repeat(32)


BF16 = ml_dtypes.bfloat16


def bf(x):
    return np.asarray(x, np.float32).astype(BF16)


def f64(x):
    return np.asarray(x).astype(np.float64)


B, C, HD, H, W = 2, 512, 128, 16, 32
N = H * W
T = B * N
C2 = 2 * C
C3 = 3 * C


def sigmoid(v):
    return 1.0 / (1.0 + np.exp(-v))


def setup_inputs():
    s = mx_kscale(T).reshape(B, 1, H, W)
    u = mx_kscale(C)
    z0 = bf(np.random.standard_normal((B, C2, H, W)))
    h0 = bf(np.random.standard_normal((B, C, H, W)))
    m = bf(np.random.standard_normal((B, C, H, W)))
    w0 = bf(np.random.standard_normal((C3, C3)) * 1.5 / np.sqrt(C3))
    bm = bf(np.random.standard_normal(C3) * 0.3)
    x0 = np.concatenate([f64(z0), f64(h0)], axis=1).reshape(B, C3, N)
    combined = (f64(w0) @ x0 + f64(bm)[None, :, None]).reshape(B, C3, H, W)
    ug = u[None, :, None, None]
    g0 = bf(4.0 * np.random.standard_normal((B, C, H, W)) * np.exp2(np.random.randint(-6, 1, (B, 1, H, W))) / s * ug)
    g1 = bf(4.0 * np.random.standard_normal((B, C, H, W)) * np.exp2(np.random.randint(-6, 1, (B, 1, H, W))) / s * ug)
    return {
        "z": bf(f64(z0) * s),
        "h": bf(f64(h0) * s),
        "m": m,
        "Wm": bf(f64(w0) / np.tile(u, 3)[:, None]),
        "bm": bm,
        "combined": np.asarray(combined, np.float32),
        "grad_0": g0,
        "grad_1": g1,
    }


def reference(z, h, m, Wm, bm, combined, grad_0, grad_1):
    cf = f64(combined)
    mf = f64(m)
    so = sigmoid(cf[:, :C])
    t = np.tanh(cf[:, C:C2])
    g = sigmoid(cf[:, C2:])
    new_m = (1.0 - g) * mf + g * t
    g0 = f64(grad_0)
    dm = f64(grad_1) + g0 * so
    dmo = g0 * new_m * so * (1.0 - so)
    dmg = dm * g * (1.0 - t * t)
    dmi = dm * (t - mf) * g * (1.0 - g)
    dc = np.concatenate([dmo, dmg, dmi], axis=1).reshape(B, C3, N).transpose(1, 0, 2).reshape(C3, T)
    x = np.concatenate([f64(z), f64(h)], axis=1).reshape(B, C3, N).transpose(1, 0, 2).reshape(C3, T)
    dx = mxq(f64(Wm), 0, "e4m3").T @ mxq(dc, 0, "e5m2")
    dw = mxq(dc, 1, "e5m2") @ mxq(x, 1, "e4m3").T
    dx = dx.reshape(C3, B, H, W).transpose(1, 0, 2, 3)
    return dx[:, :C2], dx[:, C2:], dw

@@ -1,0 +1,413 @@
+from contextlib import ExitStack
+
+import concourse.mybir as mybir
+from concourse.masks import make_identity
+
+F32 = mybir.dt.float32
+BF16 = mybir.dt.bfloat16
+U32 = mybir.dt.uint32
+U8 = mybir.dt.uint8
+E4M3 = mybir.dt.float8_e4m3fn_x4
+E5M2 = mybir.dt.float8_e5m2_x4
+ACT = mybir.ActivationFunctionType
+ALU = mybir.AluOpType
+
+P = 128
+PACK = 4
+B = 2
+N = 512
+C = 512
+GATES = 3
+C3 = GATES * C
+CT = C3 // P
+FLOPS = 2 * 2 * C3 * C3 * B * N
+BYTES = 2 * B * N * (2 * C + C + C + C + C) + 2 * C3 * C3 + 4 * B * N * C3 * 2 + 4 * C3 * C3
+
+CELLS = [(0, 0), (0, 1), (1, 0), (1, 1), (2, 0), (3, 0), (2, 1), (3, 1)]
+
+
+def tile_self_attention_memory_module_pb_v_kernel(
+    tc, z, h, m, Wm, bm, combined, grad_0, grad_1, out_0, out_1, out_2
+):
+    nc = tc.nc
+    with ExitStack() as ctx:
+        sb = ctx.enter_context(tc.tile_pool(name="sb", bufs=1))
+        ps = ctx.enter_context(tc.psum_pool(name="ps", bufs=1))
+        ctx.enter_context(tc.manual_schedule())
+
+        free_banks = list(range(8))
+
+        def take_bank():
+            i = free_banks[0]
+            free_banks.remove(i)
+            return i, ps.tile([P, N], F32, name="bank%d" % i)
+
+        ident = sb.tile([P, P], F32, name="ident")
+        make_identity(nc, ident[:])
+
+        comb = {}
+        side = {}
+        raw = {}
+        acts = {}
+        tmp = {}
+        dc = {}
+        for b in range(B):
+            for g in range(GATES):
+                dc[b, g] = sb.tile([P, PACK * N], BF16, name="dc%d%d" % (b, g), align_bytes=64)
+        stage = {}
+        dct = {}
+        xt = {}
+        dcf = {}
+        wq = {}
+
+        def comb_view(k):
+            j, b = CELLS[k]
+            return combined[b].rearrange("(g p j) y x -> p g j (y x)", g=GATES, j=PACK)[:, :, j, :]
+
+        def load_comb(k):
+            comb[k] = sb.tile([P, GATES * N], F32, name="comb", bufs=4)
+            nc.sync.dma_start(out=comb[k][:].rearrange("p (g n) -> p g n", g=GATES), in_=comb_view(k))
+
+        def load_side(name, src, b, half):
+            side[name, b, half] = sb.tile([P, 2 * N], BF16, name="side_%s%d%d" % (name, b, half))
+            view = src[b].rearrange("(p j) y x -> p (j y x)", j=PACK)
+            nc.sync.dma_start(out=side[name, b, half][:], in_=view[:, half * 2 * N : (half + 1) * 2 * N])
+
+        def load_sides(b, half):
+            load_side("g0", grad_0, b, half)
+            load_side("m", m, b, half)
+            load_side("g1", grad_1, b, half)
+
+        def load_x(b, cg):
+            src = z[b, cg * C : (cg + 1) * C] if cg < 2 else h[b]
+            nc.sync.dma_start(
+                out=raw["x", b][:, cg * 4 * N : (cg + 1) * 4 * N].rearrange("p (q r) -> p q r", q=2),
+                in_=src.rearrange("(q p i) y x -> p q (i y x)", q=2, i=2),
+            )
+
+        def load_w(g):
+            raw["w", g] = sb.tile([P, PACK * C3], BF16, name="raw", bufs=3, align_bytes=256)
+            nc.sync.dma_start(
+                out=raw["w", g][:], in_=Wm[g * C : (g + 1) * C, :].rearrange("(p j) c -> p (j c)", j=PACK)
+            )
+
+        def activate(k, name):
+            acts[k, name] = sb.tile([P, N], F32, name="act_" + name, bufs=2)
+            out = acts[k, name][:]
+            if name == "so":
+                nc.scalar.activation(out=out, in_=comb[k][:, 0:N], func=ACT.Sigmoid)
+            elif name == "t":
+                nc.scalar.activation(out=out, in_=comb[k][:, N : 2 * N], func=ACT.Tanh)
+            elif name == "g":
+                nc.scalar.activation(out=out, in_=comb[k][:, 2 * N : 3 * N], func=ACT.Sigmoid)
+            else:
+                nc.scalar.activation(out=out, in_=acts[k, "t"][:], func=ACT.Square)
+
+        def activations(k):
+            for name in ("so", "t", "g", "tt"):
+                activate(k, name)
+
+        def cell_first(k):
+            j, b = CELLS[k]
+            cols = slice((j % 2) * N, (j % 2 + 1) * N)
+            g0 = side["g0", b, j // 2][:, cols]
+            g1 = side["g1", b, j // 2][:, cols]
+            mm = side["m", b, j // 2][:, cols]
+            so, t, g = acts[k, "so"][:], acts[k, "t"][:], acts[k, "g"][:]
+            p = sb.tile([P, N], F32, name="tmp_p")
+            a = sb.tile([P, N], F32, name="tmp_a")
+            d = sb.tile([P, N], F32, name="tmp_d")
+            tmp[k] = (p, a, d)
+            nc.vector.tensor_tensor(out=p[:], in0=so, in1=g0, op=ALU.mult)
+            nc.vector.tensor_tensor(out=a[:], in0=t, in1=mm, op=ALU.subtract)
+            nc.vector.tensor_tensor(out=d[:], in0=p[:], in1=g1, op=ALU.add)
+            nc.vector.scalar_tensor_tensor(out=a[:], in0=g, scalar=1.0, in1=a[:], op0=ALU.subtract, op1=ALU.mult)
+            nc.vector.scalar_tensor_tensor(out=d[:], in0=d[:], scalar=-1.0, in1=g, op0=ALU.mult, op1=ALU.mult)
+
+        def cell_second(k):
+            j, b = CELLS[k]
+            cols = slice(j * N, (j + 1) * N)
+            so, t, tt = acts[k, "so"][:], acts[k, "t"][:], acts[k, "tt"][:]
+            p, a, d = tmp[k]
+            nc.vector.tensor_tensor(out=t, in0=t, in1=a[:], op=ALU.add)
+            nc.vector.scalar_tensor_tensor(out=p[:], in0=so, scalar=1.0, in1=p[:], op0=ALU.subtract, op1=ALU.mult)
+            nc.vector.scalar_tensor_tensor(
+                out=dc[b, 1][:, cols], in0=tt, scalar=1.0, in1=d[:], op0=ALU.subtract, op1=ALU.mult
+            )
+            nc.vector.scalar_tensor_tensor(
+                out=dc[b, 0][:, cols], in0=p[:], scalar=-1.0, in1=t, op0=ALU.mult, op1=ALU.mult
+            )
+            nc.vector.tensor_tensor(out=dc[b, 2][:, cols], in0=d[:], in1=a[:], op=ALU.mult)
+
+        def transpose_pairs(bank, slot, words):
+            for u in range(2):
+                col = (2 * slot + u) * P
+                nc.tensor.transpose(bank[:, col : col + P], words[:, u : 2 * P : 2], ident[:])
+
+        def cell_transpose(k):
+            j, b = CELLS[k]
+            st = sb.tile([P, GATES * N], BF16, name="st3", bufs=3, align_bytes=64)
+            stage["dct", k] = st
+            held = []
+            for gates in ((1, 0), (2,)):
+                i, bank = take_bank()
+                for slot, g in enumerate(gates):
+                    transpose_pairs(bank, slot, dc[b, g][:, j * N : (j + 1) * N].bitcast(F32))
+                held.append((i, bank, len(gates)))
+            col = 0
+            for i, bank, count in held:
+                nc.scalar.copy(
+                    out=st[:, col * N : (col + count) * N].bitcast(F32).rearrange("p (s m u) -> p s m u", s=count, u=2),
+                    in_=bank[:, 0 : count * 2 * P].rearrange("p (s u m) -> p s m u", s=count, u=2),
+                )
+                col = col + count
+                free_banks.append(i)
+
+        def cell_quantize(k):
+            codes = sb.tile([P, GATES * P], U32, name="dct_codes", bufs=6, align_bytes=64)
+            scales = sb.tile([P, GATES * P], U8, name="dct_scales", bufs=6, align_bytes=64)
+            dct[CELLS[k]] = (codes, scales)
+            st = stage["dct", k]
+            for lo, hi in ((0, 2), (2, 3)):
+                nc.vector.quantize_mx(
+                    out=codes[:, lo * P : hi * P].bitcast(E5M2),
+                    scales=scales[:, lo * P : hi * P],
+                    in_=st[:, lo * N : hi * N],
+                )
+
+        def x_transpose(b, cg):
+            st = sb.tile([P, PACK * C], BF16, name="st4", bufs=3, align_bytes=64)
+            stage["x", b, cg] = st
+            for q in range(2):
+                i, bank = take_bank()
+                for slot in range(2):
+                    col = (cg * 4 + q * 2 + slot) * N
+                    transpose_pairs(bank, slot, raw["x", b][:, col : col + N].bitcast(F32))
+                nc.scalar.copy(
+                    out=st[:, q * 2 * N : (q + 1) * 2 * N].bitcast(F32).rearrange("p (m s u) -> p m s u", s=2, u=2),
+                    in_=bank[:].rearrange("p (s u m) -> p m s u", s=2, u=2),
+                )
+                free_banks.append(i)
+
+        def x_quantize(b, cg):
+            codes = sb.tile([P, C], U32, name="xt_codes%d%d" % (b, cg), align_bytes=64)
+            scales = sb.tile([P, C], U8, name="xt_scales%d%d" % (b, cg), align_bytes=64)
+            xt[b, cg] = (codes, scales)
+            nc.vector.quantize_mx(out=codes[:].bitcast(E4M3), scales=scales[:], in_=stage["x", b, cg][:])
+
+        dw_view = out_2.rearrange("(g p j) c -> p g j c", g=GATES, j=PACK)
+        gate_slot = {1: 0, 0: 1, 2: 2}
+
+        def dw_bank(j, g, cg, dst):
+            i, bank = take_bank()
+            cols = slice(gate_slot[g] * P, (gate_slot[g] + 1) * P)
+            for b in range(B):
+                nc.tensor.matmul_mx(
+                    out=bank[:],
+                    lhsT=dct[j, b][0][:, cols].bitcast(E5M2),
+                    lhsT_scale=dct[j, b][1][:, cols],
+                    rhs=xt[b, cg][0][:].bitcast(E4M3),
+                    rhs_scale=xt[b, cg][1][:],
+                    start=(b == 0),
+                    stop=(b == B - 1),
+                )
+            nc.scalar.copy(out=dst, in_=bank[:])
+            free_banks.append(i)
+
+        def dw_by_columns(j, cg):
+            res = sb.tile([P, GATES * N], F32, name="res", bufs=5)
+            for g in range(GATES):
+                dw_bank(j, g, cg, res[:, g * N : (g + 1) * N])
+            nc.sync.dma_start(
+                out=dw_view[:, :, j, cg * C : (cg + 1) * C], in_=res[:].rearrange("p (g n) -> p g n", g=GATES)
+            )
+
+        def dw_by_gate(j, g):
+            res = sb.tile([P, GATES * N], F32, name="res", bufs=5)
+            for cg in range(GATES):
+                dw_bank(j, g, cg, res[:, cg * N : (cg + 1) * N])
+            nc.sync.dma_start(out=dw_view[:, g, j, :], in_=res[:])
+
+        def interleave(engine, dst, src):
+            out = dst.rearrange("p (c i t) -> p c t i", i=4, t=PACK)
+            in_ = src.rearrange("p t (c i) -> p c t i", i=4)
+            if engine == "vector":
+                nc.vector.tensor_copy(out=out, in_=in_)
+            else:
+                nc.scalar.copy(out=out, in_=in_)
+
+        def dc_interleave(b, g, engine="vector"):
+            st = sb.tile([P, PACK * N], BF16, name="st4", bufs=3, align_bytes=64)
+            stage["dcf", b, g] = st
+            interleave(engine, st[:], dc[b, g][:].rearrange("p (t n) -> p t n", t=PACK))
+
+        def dc_quantize(b, g):
+            codes = sb.tile([P, N], U32, name="dcf_codes%d%d" % (b, g), align_bytes=64)
+            scales = sb.tile([P, N], U8, name="dcf_scales%d%d" % (b, g), align_bytes=64)
+            dcf[b, g] = (codes, scales)
+            nc.vector.quantize_mx(out=codes[:].bitcast(E5M2), scales=scales[:], in_=stage["dcf", b, g][:])
+
+        def w_interleave(ct, engine="vector"):
+            st = sb.tile([P, GATES * PACK * P], BF16, name="st3", bufs=3, align_bytes=64)
+            stage["w", ct] = st
+            for g in range(GATES):
+                rows = raw["w", g][:].rearrange("p (t c) -> p t c", t=PACK)
+                interleave(engine, st[:, g * PACK * P : (g + 1) * PACK * P], rows[:, :, ct * P : (ct + 1) * P])
+
+        def w_quantize(ct):
+            codes = sb.tile([P, GATES * P], U32, name="w_codes", bufs=6, align_bytes=64)
+            scales = sb.tile([P, GATES * P], U8, name="w_scales", bufs=6, align_bytes=64)
+            wq[ct] = (codes, scales)
+            nc.vector.quantize_mx(out=codes[:].bitcast(E4M3), scales=scales[:], in_=stage["w", ct][:])
+
+        def dx_pass(bank, b, ct, g):
+            cols = slice(g * P, (g + 1) * P)
+            nc.tensor.matmul_mx(
+                out=bank[:],
+                lhsT=wq[ct][0][:, cols].bitcast(E4M3),
+                lhsT_scale=wq[ct][1][:, cols],
+                rhs=dcf[b, g][0][:].bitcast(E5M2),
+                rhs_scale=dcf[b, g][1][:],
+                start=(g == 0),
+                stop=(g == GATES - 1),
+            )
+
+        def dx_bank(b, ct, dst, engine="scalar"):
+            i, bank = take_bank()
+            for g in range(GATES):
+                dx_pass(bank, b, ct, g)
+            if engine == "vector":
+                nc.vector.tensor_copy(out=dst, in_=bank[:])
+            else:
+                nc.scalar.copy(out=dst, in_=bank[:])
+            free_banks.append(i)
+
+        def dx_rows(ct):
+            if ct < 2 * C // P:
+                return out_0[:, ct * P : (ct + 1) * P]
+            return out_1[:, ct * P - 2 * C : (ct + 1) * P - 2 * C]
+
+        def store_dx_pair(res, b, ct):
+            nc.sync.dma_start(
+                out=out_0[b, ct * P : (ct + 2) * P].rearrange("(s p) y x -> p s (y x)", s=2),
+                in_=res[:, 0 : 2 * N].rearrange("p (s n) -> p s n", s=2),
+            )
+
+        comb[0] = sb.tile([P, GATES * N], F32, name="comb", bufs=4)
+        for g, (name, src) in enumerate((("g0", grad_0), ("m", m), ("g1", grad_1))):
+            nc.sync.dma_start(out=comb[0][:, g * N : (g + 1) * N], in_=comb_view(0)[:, g, :])
+            load_side(name, src, 0, 0)
+        load_comb(1)
+        load_sides(1, 0)
+        load_comb(2)
+        for b in range(B):
+            raw["x", b] = sb.tile([P, PACK * C3], BF16, name="raw", bufs=3, align_bytes=256)
+        for cg in range(2):
+            for b in range(B):
+                load_x(b, cg)
+            if cg == 0:
+                load_comb(3)
+        activations(0)
+        load_comb(4)
+        load_sides(0, 1)
+        for b in range(B):
+            load_x(b, 2)
+
+        for k in range(len(CELLS)):
+            if k > 0:
+                cell_transpose(k - 1)
+            if k + 1 < len(CELLS):
+                activations(k + 1)
+            if k == 0:
+                load_comb(5)
+            if k == 1:
+                load_comb(6)
+                load_sides(1, 1)
+            if k == 2:
+                load_comb(7)
+                load_w(0)
+            if 1 <= k <= 3:
+                for b in range(B):
+                    x_transpose(b, k - 1)
+            if k == 3:
+                load_w(1)
+                load_w(2)
+            cell_first(k)
+            if k > 0:
+                cell_quantize(k - 1)
+            cell_second(k)
+            if 1 <= k <= 3:
+                for b in range(B):
+                    x_quantize(b, k - 1)
+            if 2 <= k <= 4:
+                dw_by_columns(0, k - 2)
+            if k == 4:
+                dw_by_gate(1, 0)
+            if k == 5:
+                dw_by_gate(1, 1)
+                dw_by_gate(1, 2)
+            if k == 6:
+                dc_interleave(0, 0, "scalar")
+            if k == 7:
+                for g in range(GATES):
+                    dw_by_gate(2, g)
+
+        cell_transpose(7)
+        dc_interleave(0, 1)
+        dc_quantize(0, 0)
+        cell_quantize(7)
+        for g in range(GATES):
+            dw_by_gate(3, g)
+        dc_interleave(0, 2)
+        dc_quantize(0, 1)
+        w_interleave(0)
+        dc_quantize(0, 2)
+        w_interleave(1)
+        w_quantize(0)
+        res_a = sb.tile([P, GATES * N], F32, name="res", bufs=5)
+        dx_bank(0, 0, res_a[:, 0:N])
+        w_interleave(2, "scalar")
+        dc_interleave(1, 0)
+        w_quantize(1)
+        dx_bank(0, 1, res_a[:, N : 2 * N])
+        store_dx_pair(res_a, 0, 0)
+        w_interleave(3, "scalar")
+        dc_interleave(1, 1)
+        dc_quantize(1, 0)
+        w_quantize(2)
+        res_b = sb.tile([P, GATES * N], F32, name="res", bufs=5)
+        dx_bank(0, 2, res_b[:, 0:N])
+        open_banks = {}
+        for ct in range(3):
+            open_banks[ct] = take_bank()
+            dx_pass(open_banks[ct][1], 1, ct, 0)
+        dc_interleave(1, 2)
+        dc_quantize(1, 1)
+        w_quantize(3)
+        dx_bank(0, 3, res_b[:, N : 2 * N])
+        store_dx_pair(res_b, 0, 2)
+        open_banks[3] = take_bank()
+        dx_pass(open_banks[3][1], 1, 3, 0)
+        for ct in range(4):
+            dx_pass(open_banks[ct][1], 1, ct, 1)
+        w_interleave(4)
+        dc_quantize(1, 2)
+        for pair in range(2):
+            res = sb.tile([P, GATES * N], F32, name="res", bufs=5)
+            for s in range(2):
+                i, bank = open_banks[2 * pair + s]
+                dx_pass(bank, 1, 2 * pair + s, 2)
+                nc.scalar.copy(out=res[:, s * N : (s + 1) * N], in_=bank[:])
+                free_banks.append(i)
+            store_dx_pair(res, 1, 2 * pair)
+        for ct in range(4, CT):
+            if ct + 1 < CT:
+                w_interleave(ct + 1)
+            w_quantize(ct)
+            res = sb.tile([P, GATES * N], F32, name="res", bufs=5)
+            dx_bank(0, ct, res[:, 0:N])
+            dx_bank(1, ct, res[:, N : 2 * N], "vector" if ct == CT - 1 else "scalar")
+            nc.sync.dma_start(
+                out=dx_rows(ct).rearrange("b p y x -> p b (y x)"),
+                in_=res[:, 0 : 2 * N].rearrange("p (b n) -> p b n", b=B),
+            )

@@ -23,7 +23,7 @@ CT = C3 // P
 FLOPS = 2 * 2 * C3 * C3 * B * N
 BYTES = 2 * B * N * (2 * C + C + C + C + C) + 2 * C3 * C3 + 4 * B * N * C3 * 2 + 4 * C3 * C3
 
-CELLS = [(0, 0), (0, 1), (1, 0), (1, 1), (2, 0), (3, 0), (2, 1), (3, 1)]
+CELLS = [(0, (0,)), (0, (1,)), (1, (0, 1)), (2, (0, 1)), (3, (0,)), (3, (1,)), (3, (0, 1))]
 
 
 def tile_self_attention_memory_module_pb_v_kernel(
@@ -51,32 +51,35 @@ def tile_self_attention_memory_module_pb_v_kernel(
         acts = {}
         tmp = {}
         dc = {}
-        for b in range(B):
-            for g in range(GATES):
-                dc[b, g] = sb.tile([P, PACK * N], BF16, name="dc%d%d" % (b, g), align_bytes=64)
+        for g in range(GATES):
+            dc[g] = sb.tile([P, PACK * B * N], BF16, name="dc%d" % g, align_bytes=64)
+        p_tile = sb.tile([P, B * N], F32, name="tmp_p")
+        a_tile = sb.tile([P, B * N], F32, name="tmp_a")
         stage = {}
         dct = {}
         xt = {}
         dcf = {}
         wq = {}
 
-        def comb_view(k):
-            j, b = CELLS[k]
-            return combined[b].rearrange("(g p j) y x -> p g j (y x)", g=GATES, j=PACK)[:, :, j, :]
+        def load_comb(j, g, batch=None):
+            if (j, g) not in comb:
+                comb[j, g] = sb.tile([P, B * N], F32, name="comb", bufs=9)
+            view = combined.rearrange("b (g p j) y x -> p g j b (y x)", g=GATES, j=PACK)[:, g, j]
+            if batch is None:
+                nc.sync.dma_start(out=comb[j, g][:].rearrange("p (b n) -> p b n", b=B), in_=view)
+            else:
+                nc.sync.dma_start(out=comb[j, g][:, batch * N : (batch + 1) * N], in_=view[:, batch, :])
 
-        def load_comb(k):
-            comb[k] = sb.tile([P, GATES * N], F32, name="comb", bufs=4)
-            nc.sync.dma_start(out=comb[k][:].rearrange("p (g n) -> p g n", g=GATES), in_=comb_view(k))
+        sources = {"g0": grad_0, "m": m, "g1": grad_1}
 
-        def load_side(name, src, b, half):
-            side[name, b, half] = sb.tile([P, 2 * N], BF16, name="side_%s%d%d" % (name, b, half))
-            view = src[b].rearrange("(p j) y x -> p (j y x)", j=PACK)
-            nc.sync.dma_start(out=side[name, b, half][:], in_=view[:, half * 2 * N : (half + 1) * 2 * N])
-
-        def load_sides(b, half):
-            load_side("g0", grad_0, b, half)
-            load_side("m", m, b, half)
-            load_side("g1", grad_1, b, half)
+        def load_side(name, half, batch=None):
+            if (name, half) not in side:
+                side[name, half] = sb.tile([P, B * 2 * N], BF16, name="side_%s%d" % (name, half))
+            view = sources[name].rearrange("b (p q j) y x -> p q b (j y x)", q=2, j=2)[:, half]
+            if batch is None:
+                nc.sync.dma_start(out=side[name, half][:].rearrange("p (b r) -> p b r", b=B), in_=view)
+            else:
+                nc.sync.dma_start(out=side[name, half][:, batch * 2 * N : (batch + 1) * 2 * N], in_=view[:, batch, :])
 
         def load_x(b, cg):
             src = z[b, cg * C : (cg + 1) * C] if cg < 2 else h[b]
@@ -91,103 +94,123 @@ def tile_self_attention_memory_module_pb_v_kernel(
                 out=raw["w", g][:], in_=Wm[g * C : (g + 1) * C, :].rearrange("(p j) c -> p (j c)", j=PACK)
             )
 
-        def activate(k, name):
-            acts[k, name] = sb.tile([P, N], F32, name="act_" + name, bufs=2)
-            out = acts[k, name][:]
-            if name == "so":
-                nc.scalar.activation(out=out, in_=comb[k][:, 0:N], func=ACT.Sigmoid)
-            elif name == "t":
-                nc.scalar.activation(out=out, in_=comb[k][:, N : 2 * N], func=ACT.Tanh)
-            elif name == "g":
-                nc.scalar.activation(out=out, in_=comb[k][:, 2 * N : 3 * N], func=ACT.Sigmoid)
+        def span(k):
+            batches = CELLS[k][1]
+            return slice(batches[0] * N, (batches[-1] + 1) * N)
+
+        def activate(k, step):
+            j = CELLS[k][0]
+            cols = span(k)
+            if step < GATES:
+                func = (ACT.Sigmoid, ACT.Tanh, ACT.Sigmoid)[step]
+                nc.scalar.activation(out=comb[j, step][:, cols], in_=comb[j, step][:, cols], func=func)
             else:
-                nc.scalar.activation(out=out, in_=acts[k, "t"][:], func=ACT.Square)
+                if j not in acts:
+                    acts[j] = sb.tile([P, B * N], F32, name="tt", bufs=2)
+                nc.scalar.activation(out=acts[j][:, cols], in_=comb[j, 1][:, cols], func=ACT.Square)
 
         def activations(k):
-            for name in ("so", "t", "g", "tt"):
-                activate(k, name)
+            for step in range(GATES + 1):
+                activate(k, step)
 
-        def cell_first(k):
-            j, b = CELLS[k]
-            cols = slice((j % 2) * N, (j % 2 + 1) * N)
-            g0 = side["g0", b, j // 2][:, cols]
-            g1 = side["g1", b, j // 2][:, cols]
-            mm = side["m", b, j // 2][:, cols]
-            so, t, g = acts[k, "so"][:], acts[k, "t"][:], acts[k, "g"][:]
-            p = sb.tile([P, N], F32, name="tmp_p")
-            a = sb.tile([P, N], F32, name="tmp_a")
-            d = sb.tile([P, N], F32, name="tmp_d")
-            tmp[k] = (p, a, d)
-            nc.vector.tensor_tensor(out=p[:], in0=so, in1=g0, op=ALU.mult)
-            nc.vector.tensor_tensor(out=a[:], in0=t, in1=mm, op=ALU.subtract)
-            nc.vector.tensor_tensor(out=d[:], in0=p[:], in1=g1, op=ALU.add)
-            nc.vector.scalar_tensor_tensor(out=a[:], in0=g, scalar=1.0, in1=a[:], op0=ALU.subtract, op1=ALU.mult)
-            nc.vector.scalar_tensor_tensor(out=d[:], in0=d[:], scalar=-1.0, in1=g, op0=ALU.mult, op1=ALU.mult)
+        def cell_ops(k):
+            j, batches = CELLS[k]
+            cols = span(k)
+            rows = slice(batches[0], batches[-1] + 1)
 
-        def cell_second(k):
-            j, b = CELLS[k]
-            cols = slice(j * N, (j + 1) * N)
-            so, t, tt = acts[k, "so"][:], acts[k, "t"][:], acts[k, "tt"][:]
-            p, a, d = tmp[k]
-            nc.vector.tensor_tensor(out=t, in0=t, in1=a[:], op=ALU.add)
-            nc.vector.scalar_tensor_tensor(out=p[:], in0=so, scalar=1.0, in1=p[:], op0=ALU.subtract, op1=ALU.mult)
-            nc.vector.scalar_tensor_tensor(
-                out=dc[b, 1][:, cols], in0=tt, scalar=1.0, in1=d[:], op0=ALU.subtract, op1=ALU.mult
-            )
-            nc.vector.scalar_tensor_tensor(
-                out=dc[b, 0][:, cols], in0=p[:], scalar=-1.0, in1=t, op0=ALU.mult, op1=ALU.mult
-            )
-            nc.vector.tensor_tensor(out=dc[b, 2][:, cols], in0=d[:], in1=a[:], op=ALU.mult)
+            def by_batch(ap):
+                return ap.rearrange("p (b n) -> p b n", n=N)
+
+            def side_view(name):
+                return side[name, j // 2][:].rearrange("p (b q n) -> p q b n", b=B, q=2)[:, j % 2, rows, :]
+
+            so, t, g = [by_batch(comb[j, i][:, cols]) for i in range(GATES)]
+            tt = by_batch(acts[j][:, cols])
+            p = by_batch(p_tile[:, cols])
+            a = by_batch(a_tile[:, cols])
+            dmo, dmg, dmi = [by_batch(dc[i][:, j * B * N : (j + 1) * B * N][:, cols]) for i in range(GATES)]
+
+            def two(out, in0, in1, op):
+                return lambda: nc.vector.tensor_tensor(out=out, in0=in0, in1=in1, op=op)
+
+            def scaled(out, in0, scalar, op0, in1):
+                return lambda: nc.vector.scalar_tensor_tensor(
+                    out=out, in0=in0, scalar=scalar, in1=in1, op0=op0, op1=ALU.mult
+                )
+
+            return [
+                two(p, so, side_view("g0"), ALU.mult),
+                two(a, t, side_view("m"), ALU.subtract),
+                scaled(so, so, 1.0, ALU.subtract, p),
+                scaled(a, g, 1.0, ALU.subtract, a),
+                two(p, p, side_view("g1"), ALU.add),
+                two(t, t, a, ALU.add),
+                scaled(p, p, -1.0, ALU.mult, g),
+                scaled(dmo, so, -1.0, ALU.mult, t),
+                scaled(dmg, tt, 1.0, ALU.subtract, p),
+                two(dmi, p, a, ALU.mult),
+            ]
 
         def transpose_pairs(bank, slot, words):
             for u in range(2):
                 col = (2 * slot + u) * P
                 nc.tensor.transpose(bank[:, col : col + P], words[:, u : 2 * P : 2], ident[:])
 
-        def cell_transpose(k):
-            j, b = CELLS[k]
-            st = sb.tile([P, GATES * N], BF16, name="st3", bufs=3, align_bytes=64)
-            stage["dct", k] = st
-            held = []
-            for gates in ((1, 0), (2,)):
-                i, bank = take_bank()
-                for slot, g in enumerate(gates):
-                    transpose_pairs(bank, slot, dc[b, g][:, j * N : (j + 1) * N].bitcast(F32))
-                held.append((i, bank, len(gates)))
-            col = 0
-            for i, bank, count in held:
+        waiting = []
+
+        def empty(count, skip=0):
+            for item in waiting[skip : skip + count]:
+                waiting.remove(item)
+                item[1]()
+                free_banks.append(item[0])
+
+        half_done = {}
+
+        def dc_transpose(j, g, batches=(0, 1)):
+            if (j, g) not in half_done:
+                half_done[j, g] = take_bank()
+            i, bank = half_done[j, g]
+            for b in batches:
+                col = (j * B + b) * N
+                transpose_pairs(bank, b, dc[g][:, col : col + N].bitcast(F32))
+
+            def copy_out():
+                st = sb.tile([P, B * N], BF16, name="st2", bufs=3, align_bytes=64)
+                stage["dct", j, g] = st
                 nc.scalar.copy(
-                    out=st[:, col * N : (col + count) * N].bitcast(F32).rearrange("p (s m u) -> p s m u", s=count, u=2),
-                    in_=bank[:, 0 : count * 2 * P].rearrange("p (s u m) -> p s m u", s=count, u=2),
-                )
-                col = col + count
-                free_banks.append(i)
-
-        def cell_quantize(k):
-            codes = sb.tile([P, GATES * P], U32, name="dct_codes", bufs=6, align_bytes=64)
-            scales = sb.tile([P, GATES * P], U8, name="dct_scales", bufs=6, align_bytes=64)
-            dct[CELLS[k]] = (codes, scales)
-            st = stage["dct", k]
-            for lo, hi in ((0, 2), (2, 3)):
-                nc.vector.quantize_mx(
-                    out=codes[:, lo * P : hi * P].bitcast(E5M2),
-                    scales=scales[:, lo * P : hi * P],
-                    in_=st[:, lo * N : hi * N],
+                    out=st[:].bitcast(F32).rearrange("p (s m u) -> p s m u", s=B, u=2),
+                    in_=bank[:].rearrange("p (s u m) -> p s m u", s=B, u=2),
                 )
 
-        def x_transpose(b, cg):
-            st = sb.tile([P, PACK * C], BF16, name="st4", bufs=3, align_bytes=64)
-            stage["x", b, cg] = st
-            for q in range(2):
-                i, bank = take_bank()
-                for slot in range(2):
-                    col = (cg * 4 + q * 2 + slot) * N
-                    transpose_pairs(bank, slot, raw["x", b][:, col : col + N].bitcast(F32))
+            if batches[-1] == B - 1:
+                waiting.append((i, copy_out))
+
+        def dct_quantize(j, g):
+            codes = sb.tile([P, B * P], U32, name="dct_codes", bufs=3, align_bytes=64)
+            scales = sb.tile([P, B * P], U8, name="dct_scales", bufs=3, align_bytes=64)
+            dct[j, g] = (codes, scales)
+            nc.vector.quantize_mx(out=codes[:].bitcast(E5M2), scales=scales[:], in_=stage["dct", j, g][:])
+
+        def x_transpose_half(b, cg, q):
+            i, bank = take_bank()
+            for slot in range(2):
+                col = (cg * 4 + q * 2 + slot) * N
+                transpose_pairs(bank, slot, raw["x", b][:, col : col + N].bitcast(F32))
+
+            def copy_out():
+                if q == 0:
+                    stage["x", b, cg] = sb.tile([P, PACK * C], BF16, name="st4", bufs=3, align_bytes=64)
+                st = stage["x", b, cg]
                 nc.scalar.copy(
                     out=st[:, q * 2 * N : (q + 1) * 2 * N].bitcast(F32).rearrange("p (m s u) -> p m s u", s=2, u=2),
                     in_=bank[:].rearrange("p (s u m) -> p m s u", s=2, u=2),
                 )
-                free_banks.append(i)
+
+            waiting.append((i, copy_out))
+
+        def x_transpose(b, cg):
+            for q in range(2):
+                x_transpose_half(b, cg, q)
 
         def x_quantize(b, cg):
             codes = sb.tile([P, C], U32, name="xt_codes%d%d" % (b, cg), align_bytes=64)
@@ -196,37 +219,44 @@ def tile_self_attention_memory_module_pb_v_kernel(
             nc.vector.quantize_mx(out=codes[:].bitcast(E4M3), scales=scales[:], in_=stage["x", b, cg][:])
 
         dw_view = out_2.rearrange("(g p j) c -> p g j c", g=GATES, j=PACK)
-        gate_slot = {1: 0, 0: 1, 2: 2}
+        results = {}
 
-        def dw_bank(j, g, cg, dst):
+        def dw_multiply(j, g, cg):
             i, bank = take_bank()
-            cols = slice(gate_slot[g] * P, (gate_slot[g] + 1) * P)
             for b in range(B):
+                cols = slice(b * P, (b + 1) * P)
                 nc.tensor.matmul_mx(
                     out=bank[:],
-                    lhsT=dct[j, b][0][:, cols].bitcast(E5M2),
-                    lhsT_scale=dct[j, b][1][:, cols],
+                    lhsT=dct[j, g][0][:, cols].bitcast(E5M2),
+                    lhsT_scale=dct[j, g][1][:, cols],
                     rhs=xt[b, cg][0][:].bitcast(E4M3),
                     rhs_scale=xt[b, cg][1][:],
                     start=(b == 0),
                     stop=(b == B - 1),
                 )
-            nc.scalar.copy(out=dst, in_=bank[:])
-            free_banks.append(i)
 
-        def dw_by_columns(j, cg):
-            res = sb.tile([P, GATES * N], F32, name="res", bufs=5)
+            def copy_out():
+                key, slot = ((j, cg), g) if j == 0 else ((j, g), cg)
+                if slot == 0:
+                    results[key] = sb.tile([P, GATES * N], F32, name="res", bufs=5)
+                res = results[key]
+                nc.scalar.copy(out=res[:, slot * N : (slot + 1) * N], in_=bank[:])
+                if slot == GATES - 1 and j == 0:
+                    nc.sync.dma_start(
+                        out=dw_view[:, :, j, cg * C : (cg + 1) * C], in_=res[:].rearrange("p (g n) -> p g n", g=GATES)
+                    )
+                elif slot == GATES - 1:
+                    nc.sync.dma_start(out=dw_view[:, g, j, :], in_=res[:])
+
+            waiting.append((i, copy_out))
+
+        def dw_columns(cg):
             for g in range(GATES):
-                dw_bank(j, g, cg, res[:, g * N : (g + 1) * N])
-            nc.sync.dma_start(
-                out=dw_view[:, :, j, cg * C : (cg + 1) * C], in_=res[:].rearrange("p (g n) -> p g n", g=GATES)
-            )
+                dw_multiply(0, g, cg)
 
-        def dw_by_gate(j, g):
-            res = sb.tile([P, GATES * N], F32, name="res", bufs=5)
+        def dw_gate(j, g):
             for cg in range(GATES):
-                dw_bank(j, g, cg, res[:, cg * N : (cg + 1) * N])
-            nc.sync.dma_start(out=dw_view[:, g, j, :], in_=res[:])
+                dw_multiply(j, g, cg)
 
         def interleave(engine, dst, src):
             out = dst.rearrange("p (c i t) -> p c t i", i=4, t=PACK)
@@ -239,7 +269,7 @@ def tile_self_attention_memory_module_pb_v_kernel(
         def dc_interleave(b, g, engine="vector"):
             st = sb.tile([P, PACK * N], BF16, name="st4", bufs=3, align_bytes=64)
             stage["dcf", b, g] = st
-            interleave(engine, st[:], dc[b, g][:].rearrange("p (t n) -> p t n", t=PACK))
+            interleave(engine, st[:], dc[g][:].rearrange("p (t b n) -> p b t n", t=PACK, b=B)[:, b])
 
         def dc_quantize(b, g):
             codes = sb.tile([P, N], U32, name="dcf_codes%d%d" % (b, g), align_bytes=64)
@@ -247,167 +277,204 @@ def tile_self_attention_memory_module_pb_v_kernel(
             dcf[b, g] = (codes, scales)
             nc.vector.quantize_mx(out=codes[:].bitcast(E5M2), scales=scales[:], in_=stage["dcf", b, g][:])
 
-        def w_interleave(ct, engine="vector"):
-            st = sb.tile([P, GATES * PACK * P], BF16, name="st3", bufs=3, align_bytes=64)
-            stage["w", ct] = st
-            for g in range(GATES):
+        def w_interleave(ct, gates):
+            if gates[0] == 0:
+                stage["w", ct] = sb.tile([P, GATES * PACK * P], BF16, name="st3", bufs=3, align_bytes=64)
+            st = stage["w", ct]
+            for g in gates:
                 rows = raw["w", g][:].rearrange("p (t c) -> p t c", t=PACK)
-                interleave(engine, st[:, g * PACK * P : (g + 1) * PACK * P], rows[:, :, ct * P : (ct + 1) * P])
+                interleave("vector", st[:, g * PACK * P : (g + 1) * PACK * P], rows[:, :, ct * P : (ct + 1) * P])
 
         def w_quantize(ct):
-            codes = sb.tile([P, GATES * P], U32, name="w_codes", bufs=6, align_bytes=64)
-            scales = sb.tile([P, GATES * P], U8, name="w_scales", bufs=6, align_bytes=64)
-            wq[ct] = (codes, scales)
+            codes = sb.tile([P, GATES * P], U32, name="w_codes", bufs=4, align_bytes=64)
+            scales = sb.tile([P, GATES * P], U8, name="w_scales", bufs=4, align_bytes=64)
             nc.vector.quantize_mx(out=codes[:].bitcast(E4M3), scales=scales[:], in_=stage["w", ct][:])
+            for g in range(GATES):
+                cols = slice(g * P, (g + 1) * P)
+                wq[ct, g] = (codes[:, cols], scales[:, cols])
 
-        def dx_pass(bank, b, ct, g):
-            cols = slice(g * P, (g + 1) * P)
+        dx_banks = {}
+
+        def dx_pass(b, ct, g, engine="scalar"):
+            if g == 0:
+                dx_banks[b, ct] = take_bank()
+            i, bank = dx_banks[b, ct]
             nc.tensor.matmul_mx(
                 out=bank[:],
-                lhsT=wq[ct][0][:, cols].bitcast(E4M3),
-                lhsT_scale=wq[ct][1][:, cols],
+                lhsT=wq[ct, g][0].bitcast(E4M3),
+                lhsT_scale=wq[ct, g][1],
                 rhs=dcf[b, g][0][:].bitcast(E5M2),
                 rhs_scale=dcf[b, g][1][:],
                 start=(g == 0),
                 stop=(g == GATES - 1),
             )
 
-        def dx_bank(b, ct, dst, engine="scalar"):
-            i, bank = take_bank()
+            def copy_out():
+                rows = out_0[:, ct * P : (ct + 1) * P] if ct < 8 else out_1[:, (ct - 8) * P : (ct - 7) * P]
+                dst = rows.rearrange("b p y x -> p b (y x)")
+                key, slot, count = ("dx", ct), b, B
+                if ct == CT - 1:
+                    key, slot, count = ("dx", ct, b), 0, 1
+                    dst = dst[:, b : b + 1, :]
+                if slot == 0:
+                    results[key] = sb.tile([P, GATES * N], F32, name="res", bufs=5)
+                res = results[key]
+                if engine == "vector":
+                    nc.vector.tensor_copy(out=res[:, slot * N : (slot + 1) * N], in_=bank[:])
+                else:
+                    nc.scalar.copy(out=res[:, slot * N : (slot + 1) * N], in_=bank[:])
+                if slot == count - 1:
+                    nc.sync.dma_start(out=dst, in_=res[:, 0 : count * N].rearrange("p (s n) -> p s n", s=count))
+
+            if g == GATES - 1:
+                waiting.append((i, copy_out))
+
+        def dx_multiply(b, ct, engine="scalar"):
             for g in range(GATES):
-                dx_pass(bank, b, ct, g)
-            if engine == "vector":
-                nc.vector.tensor_copy(out=dst, in_=bank[:])
-            else:
-                nc.scalar.copy(out=dst, in_=bank[:])
-            free_banks.append(i)
+                dx_pass(b, ct, g, engine)
 
-        def dx_rows(ct):
-            if ct < 2 * C // P:
-                return out_0[:, ct * P : (ct + 1) * P]
-            return out_1[:, ct * P - 2 * C : (ct + 1) * P - 2 * C]
-
-        def store_dx_pair(res, b, ct):
-            nc.sync.dma_start(
-                out=out_0[b, ct * P : (ct + 2) * P].rearrange("(s p) y x -> p s (y x)", s=2),
-                in_=res[:, 0 : 2 * N].rearrange("p (s n) -> p s n", s=2),
-            )
-
-        comb[0] = sb.tile([P, GATES * N], F32, name="comb", bufs=4)
-        for g, (name, src) in enumerate((("g0", grad_0), ("m", m), ("g1", grad_1))):
-            nc.sync.dma_start(out=comb[0][:, g * N : (g + 1) * N], in_=comb_view(0)[:, g, :])
-            load_side(name, src, 0, 0)
-        load_comb(1)
-        load_sides(1, 0)
-        load_comb(2)
         for b in range(B):
             raw["x", b] = sb.tile([P, PACK * C3], BF16, name="raw", bufs=3, align_bytes=256)
-        for cg in range(2):
+        for b in range(B):
+            for g, name in enumerate(("g0", "m", "g1")):
+                load_comb(0, g, b)
+                load_side(name, 0, b)
+            if b == 0:
+                load_x(0, 0)
+                load_x(1, 0)
+        for g in range(GATES):
+            load_comb(1, g)
+        for cg in range(1, GATES):
             for b in range(B):
                 load_x(b, cg)
-            if cg == 0:
-                load_comb(3)
+        for g, name in enumerate(("g0", "m", "g1")):
+            load_comb(2, g)
+            load_side(name, 1)
         activations(0)
-        load_comb(4)
-        load_sides(0, 1)
         for b in range(B):
-            load_x(b, 2)
-
-        for k in range(len(CELLS)):
-            if k > 0:
-                cell_transpose(k - 1)
-            if k + 1 < len(CELLS):
-                activations(k + 1)
-            if k == 0:
-                load_comb(5)
-            if k == 1:
-                load_comb(6)
-                load_sides(1, 1)
-            if k == 2:
-                load_comb(7)
-                load_w(0)
-            if 1 <= k <= 3:
-                for b in range(B):
-                    x_transpose(b, k - 1)
-            if k == 3:
-                load_w(1)
-                load_w(2)
-            cell_first(k)
-            if k > 0:
-                cell_quantize(k - 1)
-            cell_second(k)
-            if 1 <= k <= 3:
-                for b in range(B):
-                    x_quantize(b, k - 1)
-            if 2 <= k <= 4:
-                dw_by_columns(0, k - 2)
-            if k == 4:
-                dw_by_gate(1, 0)
-            if k == 5:
-                dw_by_gate(1, 1)
-                dw_by_gate(1, 2)
-            if k == 6:
-                dc_interleave(0, 0, "scalar")
-            if k == 7:
-                for g in range(GATES):
-                    dw_by_gate(2, g)
-
-        cell_transpose(7)
-        dc_interleave(0, 1)
-        dc_quantize(0, 0)
-        cell_quantize(7)
+            x_transpose(b, 0)
+        for step in range(GATES + 1):
+            activate(1, step)
+            empty(1)
+        for op in cell_ops(0):
+            op()
         for g in range(GATES):
-            dw_by_gate(3, g)
-        dc_interleave(0, 2)
-        dc_quantize(0, 1)
-        w_interleave(0)
-        dc_quantize(0, 2)
-        w_interleave(1)
-        w_quantize(0)
-        res_a = sb.tile([P, GATES * N], F32, name="res", bufs=5)
-        dx_bank(0, 0, res_a[:, 0:N])
-        w_interleave(2, "scalar")
+            dc_transpose(0, g, (0,))
+        activations(2)
+        for op in cell_ops(1):
+            op()
+        for g in range(GATES):
+            load_comb(3, g)
+        load_w(0)
+
+        ops = cell_ops(2)
+        for g in range(GATES):
+            dc_transpose(0, g, (1,))
+        for b in range(B):
+            x_transpose(b, 1)
+        empty(3)
+        ops[0]()
+        x_quantize(0, 0)
+        ops[1]()
+        x_quantize(1, 0)
+        ops[2]()
+        for g in range(GATES):
+            dct_quantize(0, g)
+        dw_columns(0)
+        empty(4)
+        for b in range(B):
+            x_transpose(b, 2)
+        load_w(1)
+        load_w(2)
+        ops[3]()
+        ops[4]()
+        x_quantize(0, 1)
+        ops[5]()
+        x_quantize(1, 1)
+        activate(3, 0)
+        empty(3)
+        dw_columns(1)
+        activate(3, 1)
+        empty(4)
+        activate(3, 2)
+        ops[6]()
+        ops[7]()
+        x_quantize(0, 2)
+        ops[8]()
+        x_quantize(1, 2)
+        dw_columns(2)
+        ops[9]()
+        empty(3)
+        activate(3, 3)
+
+        ops = cell_ops(3)
+        for g in range(GATES):
+            dc_transpose(1, g)
+        empty(6)
+        ops[0]()
+        ops[1]()
+        ops[2]()
+        for g in range(GATES):
+            dct_quantize(1, g)
+        activations(6)
+        for g in range(GATES):
+            dw_gate(1, g)
+            empty(3)
+        for op in ops[3:7]:
+            op()
+        for g in range(GATES):
+            ops[7 + g]()
+            dc_transpose(2, g)
+
+        ops = cell_ops(4)
+        empty(3)
+        ops[0]()
+        for g in range(GATES):
+            ops[1 + g]()
+            dct_quantize(2, g)
+        for g in range(GATES):
+            dw_gate(2, g)
+            empty(3)
+        for op in ops[4:]:
+            op()
+
+        ops = cell_ops(5)
+        for g in range(GATES):
+            dc_transpose(3, g, (0,))
+        dc_interleave(0, 0, "scalar")
+        dc_interleave(0, 1, "scalar")
+        for op in ops[:7]:
+            op()
+        for g in range(GATES):
+            ops[7 + g]()
+            dc_transpose(3, g, (1,))
+        empty(3)
+        dc_quantize(0, 0)
         dc_interleave(1, 0)
-        w_quantize(1)
-        dx_bank(0, 1, res_a[:, N : 2 * N])
-        store_dx_pair(res_a, 0, 0)
-        w_interleave(3, "scalar")
-        dc_interleave(1, 1)
+        dct_quantize(3, 0)
+        dc_quantize(0, 1)
+        dc_interleave(0, 2, "scalar")
+        dct_quantize(3, 1)
+        dct_quantize(3, 2)
         dc_quantize(1, 0)
-        w_quantize(2)
-        res_b = sb.tile([P, GATES * N], F32, name="res", bufs=5)
-        dx_bank(0, 2, res_b[:, 0:N])
-        open_banks = {}
-        for ct in range(3):
-            open_banks[ct] = take_bank()
-            dx_pass(open_banks[ct][1], 1, ct, 0)
-        dc_interleave(1, 2)
+        dc_interleave(1, 2, "scalar")
+        for g in range(GATES):
+            dw_gate(3, g)
+            empty(3)
+        w_interleave(0, (0, 1, 2))
+        dc_quantize(0, 2)
+        w_quantize(0)
+        dc_interleave(1, 1)
+        w_interleave(1, (0,))
         dc_quantize(1, 1)
-        w_quantize(3)
-        dx_bank(0, 3, res_b[:, N : 2 * N])
-        store_dx_pair(res_b, 0, 2)
-        open_banks[3] = take_bank()
-        dx_pass(open_banks[3][1], 1, 3, 0)
-        for ct in range(4):
-            dx_pass(open_banks[ct][1], 1, ct, 1)
-        w_interleave(4)
         dc_quantize(1, 2)
-        for pair in range(2):
-            res = sb.tile([P, GATES * N], F32, name="res", bufs=5)
-            for s in range(2):
-                i, bank = open_banks[2 * pair + s]
-                dx_pass(bank, 1, 2 * pair + s, 2)
-                nc.scalar.copy(out=res[:, s * N : (s + 1) * N], in_=bank[:])
-                free_banks.append(i)
-            store_dx_pair(res, 1, 2 * pair)
-        for ct in range(4, CT):
+        for ct in range(CT):
+            dx_multiply(0, ct)
+            dx_multiply(1, ct, "vector" if ct == CT - 1 else "scalar")
             if ct + 1 < CT:
-                w_interleave(ct + 1)
-            w_quantize(ct)
-            res = sb.tile([P, GATES * N], F32, name="res", bufs=5)
-            dx_bank(0, ct, res[:, 0:N])
-            dx_bank(1, ct, res[:, N : 2 * N], "vector" if ct == CT - 1 else "scalar")
-            nc.sync.dma_start(
-                out=dx_rows(ct).rearrange("b p y x -> p b (y x)"),
-                in_=res[:, 0 : 2 * N].rearrange("p (b n) -> p b n", b=B),
-            )
+                w_interleave(ct + 1, (1, 2))
+            if ct + 2 < CT:
+                w_interleave(ct + 2, (0,))
+            if ct + 1 < CT:
+                w_quantize(ct + 1)
+            empty(2)

@@ -19,11 +19,16 @@ N = 512
 C = 512
 GATES = 3
 C3 = GATES * C
-CT = C3 // P
-FLOPS = 2 * 2 * C3 * C3 * B * N
-BYTES = 2 * B * N * (2 * C + C + C + C + C) + 2 * C3 * C3 + 4 * B * N * C3 * 2 + 4 * C3 * C3
+TILES = C3 // P
+Z_TILES = 2 * C // P
+BANKS = 8
+BOTH = (0, 1)
+SIDE_INPUTS = ("grad_0", "m", "grad_1")
+RESULT_BUFS = 5
+ALIGN = 64
 
-CELLS = [(0, (0,)), (0, (1,)), (1, (0, 1)), (2, (0, 1)), (3, (0,)), (3, (1,)), (3, (0, 1))]
+FLOPS = 2 * 2 * C3 * C3 * B * N
+BYTES = 2 * B * N * 6 * C + 2 * C3 * C3 + 2 * 4 * B * N * C3 + 4 * C3 * C3
 
 
 def tile_self_attention_memory_module_pb_v_kernel(
@@ -35,87 +40,98 @@ def tile_self_attention_memory_module_pb_v_kernel(
         ps = ctx.enter_context(tc.psum_pool(name="ps", bufs=1))
         ctx.enter_context(tc.manual_schedule())
 
-        free_banks = list(range(8))
+        free_banks = list(range(BANKS))
+        filled = []
 
         def take_bank():
-            i = free_banks[0]
-            free_banks.remove(i)
-            return i, ps.tile([P, N], F32, name="bank%d" % i)
+            number = free_banks[0]
+            free_banks.remove(number)
+            return number, ps.tile([P, N], F32, name="bank%d" % number)
+
+        def empty_banks(count, skip=0):
+            for item in filled[skip : skip + count]:
+                filled.remove(item)
+                item[1]()
+                free_banks.append(item[0])
 
         ident = sb.tile([P, P], F32, name="ident")
         make_identity(nc, ident[:])
 
-        comb = {}
-        side = {}
-        raw = {}
-        acts = {}
-        tmp = {}
         dc = {}
         for g in range(GATES):
-            dc[g] = sb.tile([P, PACK * B * N], BF16, name="dc%d" % g, align_bytes=64)
+            dc[g] = sb.tile([P, PACK * B * N], BF16, name="dc%d" % g, align_bytes=ALIGN)
         p_tile = sb.tile([P, B * N], F32, name="tmp_p")
         a_tile = sb.tile([P, B * N], F32, name="tmp_a")
-        stage = {}
-        dct = {}
-        xt = {}
-        dcf = {}
-        wq = {}
+        d_tile = sb.tile([P, B * N], F32, name="tmp_d")
 
-        def load_comb(j, g, batch=None):
-            if (j, g) not in comb:
-                comb[j, g] = sb.tile([P, B * N], F32, name="comb", bufs=9)
+        gate_in = {}
+        side = {}
+        tanh_sq = {}
+        x_raw = {}
+        w_raw = {}
+        staged = {}
+        dc_tok = {}
+        x_tok = {}
+        dc_ch = {}
+        w_ch = {}
+        results = {}
+
+        def load_combined(j, g, batch=None):
+            if (j, g) not in gate_in:
+                gate_in[j, g] = sb.tile([P, B * N], F32, name="gate_in", bufs=3 * GATES)
             view = combined.rearrange("b (g p j) y x -> p g j b (y x)", g=GATES, j=PACK)[:, g, j]
             if batch is None:
-                nc.sync.dma_start(out=comb[j, g][:].rearrange("p (b n) -> p b n", b=B), in_=view)
+                nc.sync.dma_start(out=gate_in[j, g][:].rearrange("p (b n) -> p b n", b=B), in_=view)
             else:
-                nc.sync.dma_start(out=comb[j, g][:, batch * N : (batch + 1) * N], in_=view[:, batch, :])
+                nc.sync.dma_start(out=gate_in[j, g][:, batch * N : (batch + 1) * N], in_=view[:, batch, :])
 
-        sources = {"g0": grad_0, "m": m, "g1": grad_1}
+        sources = {"grad_0": grad_0, "m": m, "grad_1": grad_1}
 
-        def load_side(name, half, batch=None):
-            if (name, half) not in side:
-                side[name, half] = sb.tile([P, B * 2 * N], BF16, name="side_%s%d" % (name, half))
-            view = sources[name].rearrange("b (p q j) y x -> p q b (j y x)", q=2, j=2)[:, half]
+        def load_side(name, pair, batch=None, member=None):
+            if (name, pair) not in side:
+                side[name, pair] = sb.tile([P, B * 2 * N], BF16, name="side_%s%d" % (name, pair))
+            view = sources[name].rearrange("b (p q j) y x -> p q b j (y x)", q=2, j=2)[:, pair]
+            tile = side[name, pair][:].rearrange("p (b j n) -> p b j n", b=B, j=2)
             if batch is None:
-                nc.sync.dma_start(out=side[name, half][:].rearrange("p (b r) -> p b r", b=B), in_=view)
+                nc.sync.dma_start(out=tile.rearrange("p b j n -> p b (j n)"), in_=view.rearrange("p b j n -> p b (j n)"))
+            elif member is None:
+                nc.sync.dma_start(out=tile[:, batch], in_=view[:, batch])
             else:
-                nc.sync.dma_start(out=side[name, half][:, batch * 2 * N : (batch + 1) * 2 * N], in_=view[:, batch, :])
+                nc.sync.dma_start(out=tile[:, batch, member], in_=view[:, batch, member])
 
-        def load_x(b, cg):
-            src = z[b, cg * C : (cg + 1) * C] if cg < 2 else h[b]
+        def raw_tile():
+            return sb.tile([P, PACK * C3], BF16, name="raw", bufs=3, align_bytes=256)
+
+        def load_x(b, group):
+            src = z[b, group * C : (group + 1) * C] if group < 2 else h[b]
             nc.sync.dma_start(
-                out=raw["x", b][:, cg * 4 * N : (cg + 1) * 4 * N].rearrange("p (q r) -> p q r", q=2),
+                out=x_raw[b][:, group * 4 * N : (group + 1) * 4 * N].rearrange("p (q r) -> p q r", q=2),
                 in_=src.rearrange("(q p i) y x -> p q (i y x)", q=2, i=2),
             )
 
         def load_w(g):
-            raw["w", g] = sb.tile([P, PACK * C3], BF16, name="raw", bufs=3, align_bytes=256)
-            nc.sync.dma_start(
-                out=raw["w", g][:], in_=Wm[g * C : (g + 1) * C, :].rearrange("(p j) c -> p (j c)", j=PACK)
-            )
+            w_raw[g] = raw_tile()
+            nc.sync.dma_start(out=w_raw[g][:], in_=Wm[g * C : (g + 1) * C, :].rearrange("(p j) c -> p (j c)", j=PACK))
 
-        def span(k):
-            batches = CELLS[k][1]
+        def columns(batches):
             return slice(batches[0] * N, (batches[-1] + 1) * N)
 
-        def activate(k, step):
-            j = CELLS[k][0]
-            cols = span(k)
-            if step < GATES:
-                func = (ACT.Sigmoid, ACT.Tanh, ACT.Sigmoid)[step]
-                nc.scalar.activation(out=comb[j, step][:, cols], in_=comb[j, step][:, cols], func=func)
+        def activate(j, batches, part):
+            cols = columns(batches)
+            if part < GATES:
+                func = (ACT.Sigmoid, ACT.Tanh, ACT.Sigmoid)[part]
+                nc.scalar.activation(out=gate_in[j, part][:, cols], in_=gate_in[j, part][:, cols], func=func)
             else:
-                if j not in acts:
-                    acts[j] = sb.tile([P, B * N], F32, name="tt", bufs=2)
-                nc.scalar.activation(out=acts[j][:, cols], in_=comb[j, 1][:, cols], func=ACT.Square)
+                if j not in tanh_sq:
+                    tanh_sq[j] = sb.tile([P, B * N], F32, name="tanh_sq", bufs=2)
+                nc.scalar.activation(out=tanh_sq[j][:, cols], in_=gate_in[j, 1][:, cols], func=ACT.Square)
 
-        def activations(k):
-            for step in range(GATES + 1):
-                activate(k, step)
+        def activations(j, batches):
+            for part in range(GATES + 1):
+                activate(j, batches, part)
 
-        def cell_ops(k):
-            j, batches = CELLS[k]
-            cols = span(k)
+        def step_ops(j, batches):
+            cols = columns(batches)
             rows = slice(batches[0], batches[-1] + 1)
 
             def by_batch(ap):
@@ -124,10 +140,11 @@ def tile_self_attention_memory_module_pb_v_kernel(
             def side_view(name):
                 return side[name, j // 2][:].rearrange("p (b q n) -> p q b n", b=B, q=2)[:, j % 2, rows, :]
 
-            so, t, g = [by_batch(comb[j, i][:, cols]) for i in range(GATES)]
-            tt = by_batch(acts[j][:, cols])
+            so, t, g = [by_batch(gate_in[j, i][:, cols]) for i in range(GATES)]
+            tt = by_batch(tanh_sq[j][:, cols])
             p = by_batch(p_tile[:, cols])
             a = by_batch(a_tile[:, cols])
+            d = by_batch(d_tile[:, cols])
             dmo, dmg, dmi = [by_batch(dc[i][:, j * B * N : (j + 1) * B * N][:, cols]) for i in range(GATES)]
 
             def two(out, in0, in1, op):
@@ -139,342 +156,334 @@ def tile_self_attention_memory_module_pb_v_kernel(
                 )
 
             return [
-                two(p, so, side_view("g0"), ALU.mult),
+                two(p, so, side_view("grad_0"), ALU.mult),
                 two(a, t, side_view("m"), ALU.subtract),
                 scaled(so, so, 1.0, ALU.subtract, p),
                 scaled(a, g, 1.0, ALU.subtract, a),
-                two(p, p, side_view("g1"), ALU.add),
+                two(d, p, side_view("grad_1"), ALU.add),
                 two(t, t, a, ALU.add),
-                scaled(p, p, -1.0, ALU.mult, g),
+                scaled(d, d, -1.0, ALU.mult, g),
                 scaled(dmo, so, -1.0, ALU.mult, t),
-                scaled(dmg, tt, 1.0, ALU.subtract, p),
-                two(dmi, p, a, ALU.mult),
+                scaled(dmg, tt, 1.0, ALU.subtract, d),
+                two(dmi, d, a, ALU.mult),
             ]
 
-        def transpose_pairs(bank, slot, words):
+        def transpose_words(bank, place, words):
             for u in range(2):
-                col = (2 * slot + u) * P
+                col = (2 * place + u) * P
                 nc.tensor.transpose(bank[:, col : col + P], words[:, u : 2 * P : 2], ident[:])
 
-        waiting = []
+        dc_banks = {}
 
-        def empty(count, skip=0):
-            for item in waiting[skip : skip + count]:
-                waiting.remove(item)
-                item[1]()
-                free_banks.append(item[0])
-
-        half_done = {}
-
-        def dc_transpose(j, g, batches=(0, 1)):
-            if (j, g) not in half_done:
-                half_done[j, g] = take_bank()
-            i, bank = half_done[j, g]
+        def dc_transpose(j, g, batches):
+            if batches[0] == 0:
+                dc_banks[j, g] = take_bank()
+            number, bank = dc_banks[j, g]
             for b in batches:
                 col = (j * B + b) * N
-                transpose_pairs(bank, b, dc[g][:, col : col + N].bitcast(F32))
+                transpose_words(bank, b, dc[g][:, col : col + N].bitcast(F32))
 
             def copy_out():
-                st = sb.tile([P, B * N], BF16, name="st2", bufs=3, align_bytes=64)
-                stage["dct", j, g] = st
+                staged["dc_tok", j, g] = sb.tile([P, B * N], BF16, name="stage_dc_tok", bufs=GATES, align_bytes=ALIGN)
                 nc.scalar.copy(
-                    out=st[:].bitcast(F32).rearrange("p (s m u) -> p s m u", s=B, u=2),
+                    out=staged["dc_tok", j, g][:].bitcast(F32).rearrange("p (s m u) -> p s m u", s=B, u=2),
                     in_=bank[:].rearrange("p (s u m) -> p s m u", s=B, u=2),
                 )
 
             if batches[-1] == B - 1:
-                waiting.append((i, copy_out))
+                filled.append((number, copy_out))
 
-        def dct_quantize(j, g):
-            codes = sb.tile([P, B * P], U32, name="dct_codes", bufs=3, align_bytes=64)
-            scales = sb.tile([P, B * P], U8, name="dct_scales", bufs=3, align_bytes=64)
-            dct[j, g] = (codes, scales)
-            nc.vector.quantize_mx(out=codes[:].bitcast(E5M2), scales=scales[:], in_=stage["dct", j, g][:])
+        def dc_quantize_tokens(j, g):
+            codes = sb.tile([P, B * P], U32, name="dc_tok_codes", bufs=GATES, align_bytes=ALIGN)
+            scales = sb.tile([P, B * P], U8, name="dc_tok_scales", bufs=GATES, align_bytes=ALIGN)
+            dc_tok[j, g] = (codes, scales)
+            nc.vector.quantize_mx(out=codes[:].bitcast(E5M2), scales=scales[:], in_=staged["dc_tok", j, g][:])
 
-        def x_transpose_half(b, cg, q):
-            i, bank = take_bank()
-            for slot in range(2):
-                col = (cg * 4 + q * 2 + slot) * N
-                transpose_pairs(bank, slot, raw["x", b][:, col : col + N].bitcast(F32))
+        def wide_stage():
+            return sb.tile([P, PACK * N], BF16, name="stage_wide", bufs=3, align_bytes=ALIGN)
+
+        def x_transpose_half(b, group, q):
+            number, bank = take_bank()
+            for i in range(2):
+                col = (group * 4 + q * 2 + i) * N
+                transpose_words(bank, i, x_raw[b][:, col : col + N].bitcast(F32))
 
             def copy_out():
                 if q == 0:
-                    stage["x", b, cg] = sb.tile([P, PACK * C], BF16, name="st4", bufs=3, align_bytes=64)
-                st = stage["x", b, cg]
+                    staged["x", b, group] = wide_stage()
+                half = staged["x", b, group][:, q * 2 * N : (q + 1) * 2 * N]
                 nc.scalar.copy(
-                    out=st[:, q * 2 * N : (q + 1) * 2 * N].bitcast(F32).rearrange("p (m s u) -> p m s u", s=2, u=2),
-                    in_=bank[:].rearrange("p (s u m) -> p m s u", s=2, u=2),
+                    out=half.bitcast(F32).rearrange("p (m i u) -> p m i u", i=2, u=2),
+                    in_=bank[:].rearrange("p (i u m) -> p m i u", i=2, u=2),
                 )
 
-            waiting.append((i, copy_out))
+            filled.append((number, copy_out))
 
-        def x_transpose(b, cg):
-            for q in range(2):
-                x_transpose_half(b, cg, q)
+        def x_transpose(group):
+            for b in range(B):
+                for q in range(2):
+                    x_transpose_half(b, group, q)
 
-        def x_quantize(b, cg):
-            codes = sb.tile([P, C], U32, name="xt_codes%d%d" % (b, cg), align_bytes=64)
-            scales = sb.tile([P, C], U8, name="xt_scales%d%d" % (b, cg), align_bytes=64)
-            xt[b, cg] = (codes, scales)
-            nc.vector.quantize_mx(out=codes[:].bitcast(E4M3), scales=scales[:], in_=stage["x", b, cg][:])
+        def x_quantize(b, group):
+            codes = sb.tile([P, C], U32, name="x_codes%d%d" % (b, group), align_bytes=ALIGN)
+            scales = sb.tile([P, C], U8, name="x_scales%d%d" % (b, group), align_bytes=ALIGN)
+            x_tok[b, group] = (codes, scales)
+            nc.vector.quantize_mx(out=codes[:].bitcast(E4M3), scales=scales[:], in_=staged["x", b, group][:])
 
         dw_view = out_2.rearrange("(g p j) c -> p g j c", g=GATES, j=PACK)
-        results = {}
 
-        def dw_multiply(j, g, cg):
-            i, bank = take_bank()
+        def result_tile():
+            return sb.tile([P, GATES * N], F32, name="result", bufs=RESULT_BUFS)
+
+        def dw_multiply(j, g, group):
+            number, bank = take_bank()
             for b in range(B):
                 cols = slice(b * P, (b + 1) * P)
                 nc.tensor.matmul_mx(
                     out=bank[:],
-                    lhsT=dct[j, g][0][:, cols].bitcast(E5M2),
-                    lhsT_scale=dct[j, g][1][:, cols],
-                    rhs=xt[b, cg][0][:].bitcast(E4M3),
-                    rhs_scale=xt[b, cg][1][:],
+                    lhsT=dc_tok[j, g][0][:, cols].bitcast(E5M2),
+                    lhsT_scale=dc_tok[j, g][1][:, cols],
+                    rhs=x_tok[b, group][0][:].bitcast(E4M3),
+                    rhs_scale=x_tok[b, group][1][:],
                     start=(b == 0),
                     stop=(b == B - 1),
                 )
 
             def copy_out():
-                key, slot = ((j, cg), g) if j == 0 else ((j, g), cg)
-                if slot == 0:
-                    results[key] = sb.tile([P, GATES * N], F32, name="res", bufs=5)
-                res = results[key]
-                nc.scalar.copy(out=res[:, slot * N : (slot + 1) * N], in_=bank[:])
-                if slot == GATES - 1 and j == 0:
+                place = g if j == 0 else group
+                if place == 0:
+                    results["dw"] = result_tile()
+                res = results["dw"]
+                nc.scalar.copy(out=res[:, place * N : (place + 1) * N], in_=bank[:])
+                if place == GATES - 1 and j == 0:
                     nc.sync.dma_start(
-                        out=dw_view[:, :, j, cg * C : (cg + 1) * C], in_=res[:].rearrange("p (g n) -> p g n", g=GATES)
+                        out=dw_view[:, :, j, group * C : (group + 1) * C],
+                        in_=res[:].rearrange("p (g n) -> p g n", g=GATES),
                     )
-                elif slot == GATES - 1:
+                elif place == GATES - 1:
                     nc.sync.dma_start(out=dw_view[:, g, j, :], in_=res[:])
 
-            waiting.append((i, copy_out))
+            filled.append((number, copy_out))
 
-        def dw_columns(cg):
+        def dw_first_rows(group):
             for g in range(GATES):
-                dw_multiply(0, g, cg)
+                dw_multiply(0, g, group)
 
-        def dw_gate(j, g):
-            for cg in range(GATES):
-                dw_multiply(j, g, cg)
-
-        def interleave(engine, dst, src):
-            out = dst.rearrange("p (c i t) -> p c t i", i=4, t=PACK)
-            in_ = src.rearrange("p t (c i) -> p c t i", i=4)
-            if engine == "vector":
-                nc.vector.tensor_copy(out=out, in_=in_)
-            else:
-                nc.scalar.copy(out=out, in_=in_)
-
-        def dc_interleave(b, g, engine="vector"):
-            st = sb.tile([P, PACK * N], BF16, name="st4", bufs=3, align_bytes=64)
-            stage["dcf", b, g] = st
-            interleave(engine, st[:], dc[g][:].rearrange("p (t b n) -> p b t n", t=PACK, b=B)[:, b])
-
-        def dc_quantize(b, g):
-            codes = sb.tile([P, N], U32, name="dcf_codes%d%d" % (b, g), align_bytes=64)
-            scales = sb.tile([P, N], U8, name="dcf_scales%d%d" % (b, g), align_bytes=64)
-            dcf[b, g] = (codes, scales)
-            nc.vector.quantize_mx(out=codes[:].bitcast(E5M2), scales=scales[:], in_=stage["dcf", b, g][:])
-
-        def w_interleave(ct, gates):
-            if gates[0] == 0:
-                stage["w", ct] = sb.tile([P, GATES * PACK * P], BF16, name="st3", bufs=3, align_bytes=64)
-            st = stage["w", ct]
-            for g in gates:
-                rows = raw["w", g][:].rearrange("p (t c) -> p t c", t=PACK)
-                interleave("vector", st[:, g * PACK * P : (g + 1) * PACK * P], rows[:, :, ct * P : (ct + 1) * P])
-
-        def w_quantize(ct):
-            codes = sb.tile([P, GATES * P], U32, name="w_codes", bufs=4, align_bytes=64)
-            scales = sb.tile([P, GATES * P], U8, name="w_scales", bufs=4, align_bytes=64)
-            nc.vector.quantize_mx(out=codes[:].bitcast(E4M3), scales=scales[:], in_=stage["w", ct][:])
+        def dw_rows(j):
             for g in range(GATES):
-                cols = slice(g * P, (g + 1) * P)
-                wq[ct, g] = (codes[:, cols], scales[:, cols])
+                for group in range(GATES):
+                    dw_multiply(j, g, group)
+                empty_banks(GATES)
 
-        dx_banks = {}
-
-        def dx_pass(b, ct, g, engine="scalar"):
-            if g == 0:
-                dx_banks[b, ct] = take_bank()
-            i, bank = dx_banks[b, ct]
-            nc.tensor.matmul_mx(
-                out=bank[:],
-                lhsT=wq[ct, g][0].bitcast(E4M3),
-                lhsT_scale=wq[ct, g][1],
-                rhs=dcf[b, g][0][:].bitcast(E5M2),
-                rhs_scale=dcf[b, g][1][:],
-                start=(g == 0),
-                stop=(g == GATES - 1),
+        def interleave(copy, dst, src):
+            copy(
+                out=dst.rearrange("p (c i j) -> p c j i", i=4, j=PACK),
+                in_=src.rearrange("p j (c i) -> p c j i", i=4),
             )
 
-            def copy_out():
-                rows = out_0[:, ct * P : (ct + 1) * P] if ct < 8 else out_1[:, (ct - 8) * P : (ct - 7) * P]
-                dst = rows.rearrange("b p y x -> p b (y x)")
-                key, slot, count = ("dx", ct), b, B
-                if ct == CT - 1:
-                    key, slot, count = ("dx", ct, b), 0, 1
-                    dst = dst[:, b : b + 1, :]
-                if slot == 0:
-                    results[key] = sb.tile([P, GATES * N], F32, name="res", bufs=5)
-                res = results[key]
-                if engine == "vector":
-                    nc.vector.tensor_copy(out=res[:, slot * N : (slot + 1) * N], in_=bank[:])
-                else:
-                    nc.scalar.copy(out=res[:, slot * N : (slot + 1) * N], in_=bank[:])
-                if slot == count - 1:
-                    nc.sync.dma_start(out=dst, in_=res[:, 0 : count * N].rearrange("p (s n) -> p s n", s=count))
+        def dc_interleave(b, g, copy):
+            staged["dc_ch", b, g] = wide_stage()
+            rows = dc[g][:].rearrange("p (j b n) -> p b j n", j=PACK, b=B)[:, b]
+            interleave(copy, staged["dc_ch", b, g][:], rows)
 
-            if g == GATES - 1:
-                waiting.append((i, copy_out))
+        def dc_quantize_channels(b, g):
+            codes = sb.tile([P, N], U32, name="dc_ch_codes%d%d" % (b, g), align_bytes=ALIGN)
+            scales = sb.tile([P, N], U8, name="dc_ch_scales%d%d" % (b, g), align_bytes=ALIGN)
+            dc_ch[b, g] = (codes, scales)
+            nc.vector.quantize_mx(out=codes[:].bitcast(E5M2), scales=scales[:], in_=staged["dc_ch", b, g][:])
 
-        def dx_multiply(b, ct, engine="scalar"):
+        def w_interleave(tile, gates):
+            if gates[0] == 0:
+                staged["w", tile] = sb.tile([P, GATES * PACK * P], BF16, name="stage_w", bufs=3, align_bytes=ALIGN)
+            for g in gates:
+                rows = w_raw[g][:].rearrange("p (j c) -> p j c", j=PACK)
+                interleave(
+                    nc.vector.tensor_copy,
+                    staged["w", tile][:, g * PACK * P : (g + 1) * PACK * P],
+                    rows[:, :, tile * P : (tile + 1) * P],
+                )
+
+        def w_quantize(tile):
+            codes = sb.tile([P, GATES * P], U32, name="w_codes", bufs=3, align_bytes=ALIGN)
+            scales = sb.tile([P, GATES * P], U8, name="w_scales", bufs=3, align_bytes=ALIGN)
+            nc.vector.quantize_mx(out=codes[:].bitcast(E4M3), scales=scales[:], in_=staged["w", tile][:])
             for g in range(GATES):
-                dx_pass(b, ct, g, engine)
+                cols = slice(g * P, (g + 1) * P)
+                w_ch[tile, g] = (codes[:, cols], scales[:, cols])
+
+        def dx_multiply(b, tile, tokens, copy):
+            number, bank = take_bank()
+            width = tokens.stop - tokens.start
+            for g in range(GATES):
+                nc.tensor.matmul_mx(
+                    out=bank[:, 0:width],
+                    lhsT=w_ch[tile, g][0].bitcast(E4M3),
+                    lhsT_scale=w_ch[tile, g][1],
+                    rhs=dc_ch[b, g][0][:, tokens].bitcast(E5M2),
+                    rhs_scale=dc_ch[b, g][1][:, tokens],
+                    start=(g == 0),
+                    stop=(g == GATES - 1),
+                )
+
+            def copy_out():
+                if tile < Z_TILES:
+                    rows = out_0[:, tile * P : (tile + 1) * P]
+                else:
+                    rows = out_1[:, (tile - Z_TILES) * P : (tile - Z_TILES + 1) * P]
+                dst = rows.rearrange("b p y x -> p b (y x)")
+                if b == 0:
+                    results["dx"] = result_tile()
+                res = results["dx"][:, 0 : B * N].rearrange("p (b n) -> p b n", b=B)
+                copy(out=res[:, b, tokens], in_=bank[:, 0:width])
+                if tile >= TILES - 2:
+                    nc.sync.dma_start(out=dst[:, b, tokens], in_=res[:, b, tokens])
+                elif b == B - 1:
+                    nc.sync.dma_start(out=dst, in_=res)
+
+            filled.append((number, copy_out))
+
+        on_vector = nc.vector.tensor_copy
+        on_scalar = nc.scalar.copy
+
+        def run(ops):
+            for op in ops:
+                op()
 
         for b in range(B):
-            raw["x", b] = sb.tile([P, PACK * C3], BF16, name="raw", bufs=3, align_bytes=256)
+            x_raw[b] = raw_tile()
+        for g, name in enumerate(SIDE_INPUTS):
+            load_combined(0, g, 0)
+            load_side(name, 0, 0, 0)
         for b in range(B):
-            for g, name in enumerate(("g0", "m", "g1")):
-                load_comb(0, g, b)
-                load_side(name, 0, b)
-            if b == 0:
-                load_x(0, 0)
-                load_x(1, 0)
-        for g in range(GATES):
-            load_comb(1, g)
-        for cg in range(1, GATES):
+            load_x(b, 0)
+        for g, name in enumerate(SIDE_INPUTS):
+            load_combined(0, g, 1)
+            load_side(name, 0, 1)
+        for g, name in enumerate(SIDE_INPUTS):
+            load_combined(1, g)
+            load_side(name, 0, 0, 1)
+        for group in range(1, GATES):
             for b in range(B):
-                load_x(b, cg)
-        for g, name in enumerate(("g0", "m", "g1")):
-            load_comb(2, g)
+                load_x(b, group)
+        for g, name in enumerate(SIDE_INPUTS):
+            load_combined(2, g)
             load_side(name, 1)
-        activations(0)
-        for b in range(B):
-            x_transpose(b, 0)
-        for step in range(GATES + 1):
-            activate(1, step)
-            empty(1)
-        for op in cell_ops(0):
-            op()
+
+        activations(0, (0,))
+        x_transpose(0)
+        for part in range(GATES + 1):
+            empty_banks(1)
+            activate(0, (1,), part)
+        run(step_ops(0, (0,)))
         for g in range(GATES):
             dc_transpose(0, g, (0,))
-        activations(2)
-        for op in cell_ops(1):
-            op()
+        activations(1, BOTH)
+        run(step_ops(0, (1,)))
         for g in range(GATES):
-            load_comb(3, g)
-        load_w(0)
+            load_combined(3, g)
 
-        ops = cell_ops(2)
+        ops = step_ops(1, BOTH)
         for g in range(GATES):
             dc_transpose(0, g, (1,))
+        x_transpose(1)
+        empty_banks(GATES)
         for b in range(B):
-            x_transpose(b, 1)
-        empty(3)
-        ops[0]()
-        x_quantize(0, 0)
-        ops[1]()
-        x_quantize(1, 0)
+            ops[b]()
+            x_quantize(b, 0)
         ops[2]()
         for g in range(GATES):
-            dct_quantize(0, g)
-        dw_columns(0)
-        empty(4)
-        for b in range(B):
-            x_transpose(b, 2)
-        load_w(1)
-        load_w(2)
+            dc_quantize_tokens(0, g)
+        dw_first_rows(0)
+        empty_banks(2 * B)
+        x_transpose(2)
         ops[3]()
-        ops[4]()
-        x_quantize(0, 1)
-        ops[5]()
-        x_quantize(1, 1)
-        activate(3, 0)
-        empty(3)
-        dw_columns(1)
-        activate(3, 1)
-        empty(4)
-        activate(3, 2)
+        for b in range(B):
+            ops[4 + b]()
+            x_quantize(b, 1)
+        activate(2, BOTH, 0)
+        empty_banks(GATES)
+        load_w(0)
+        dw_first_rows(1)
+        activate(2, BOTH, 1)
+        empty_banks(2 * B)
+        activate(2, BOTH, 2)
         ops[6]()
-        ops[7]()
-        x_quantize(0, 2)
-        ops[8]()
-        x_quantize(1, 2)
-        dw_columns(2)
+        for b in range(B):
+            ops[7 + b]()
+            x_quantize(b, 2)
+        dw_first_rows(2)
         ops[9]()
-        empty(3)
-        activate(3, 3)
+        empty_banks(GATES)
+        load_w(1)
+        activate(2, BOTH, 3)
 
-        ops = cell_ops(3)
+        ops = step_ops(2, BOTH)
         for g in range(GATES):
-            dc_transpose(1, g)
-        empty(6)
-        ops[0]()
-        ops[1]()
-        ops[2]()
+            dc_transpose(1, g, BOTH)
+        empty_banks(GATES, skip=GATES)
+        empty_banks(GATES)
+        load_w(2)
+        run(ops[:2])
+        activations(3, (0,))
         for g in range(GATES):
-            dct_quantize(1, g)
-        activations(6)
-        for g in range(GATES):
-            dw_gate(1, g)
-            empty(3)
-        for op in ops[3:7]:
-            op()
+            ops[2 + g]()
+            dc_quantize_tokens(1, g)
+        dw_rows(1)
+        run(ops[5:7])
         for g in range(GATES):
             ops[7 + g]()
-            dc_transpose(2, g)
+            dc_transpose(2, g, BOTH)
 
-        ops = cell_ops(4)
-        empty(3)
-        ops[0]()
+        ops = step_ops(3, (0,))
+        empty_banks(GATES)
+        activations(3, (1,))
+        run(ops[:2])
         for g in range(GATES):
-            ops[1 + g]()
-            dct_quantize(2, g)
-        for g in range(GATES):
-            dw_gate(2, g)
-            empty(3)
-        for op in ops[4:]:
-            op()
+            ops[2 + g]()
+            dc_quantize_tokens(2, g)
+        dw_rows(2)
+        run(ops[5:])
 
-        ops = cell_ops(5)
+        ops = step_ops(3, (1,))
         for g in range(GATES):
             dc_transpose(3, g, (0,))
-        dc_interleave(0, 0, "scalar")
-        dc_interleave(0, 1, "scalar")
-        for op in ops[:7]:
-            op()
+        dc_interleave(0, 0, on_scalar)
+        run(ops[:7])
         for g in range(GATES):
             ops[7 + g]()
             dc_transpose(3, g, (1,))
-        empty(3)
-        dc_quantize(0, 0)
-        dc_interleave(1, 0)
-        dct_quantize(3, 0)
-        dc_quantize(0, 1)
-        dc_interleave(0, 2, "scalar")
-        dct_quantize(3, 1)
-        dct_quantize(3, 2)
-        dc_quantize(1, 0)
-        dc_interleave(1, 2, "scalar")
-        for g in range(GATES):
-            dw_gate(3, g)
-            empty(3)
-        w_interleave(0, (0, 1, 2))
-        dc_quantize(0, 2)
+        empty_banks(GATES)
+
+        dc_quantize_channels(0, 0)
+        dc_interleave(0, 1, on_vector)
+        dc_quantize_tokens(3, 0)
+        dc_interleave(1, 0, on_vector)
+        dc_quantize_channels(0, 1)
+        dc_interleave(0, 2, on_scalar)
+        dc_quantize_tokens(3, 1)
+        dc_quantize_tokens(3, 2)
+        dc_quantize_channels(1, 0)
+        dc_interleave(1, 2, on_scalar)
+        dw_rows(3)
+        w_interleave(0, range(GATES))
+        dc_quantize_channels(0, 2)
         w_quantize(0)
-        dc_interleave(1, 1)
+        dc_interleave(1, 1, on_vector)
         w_interleave(1, (0,))
-        dc_quantize(1, 1)
-        dc_quantize(1, 2)
-        for ct in range(CT):
-            dx_multiply(0, ct)
-            dx_multiply(1, ct, "vector" if ct == CT - 1 else "scalar")
-            if ct + 1 < CT:
-                w_interleave(ct + 1, (1, 2))
-            if ct + 2 < CT:
-                w_interleave(ct + 2, (0,))
-            if ct + 1 < CT:
-                w_quantize(ct + 1)
-            empty(2)
+        dc_quantize_channels(1, 1)
+        dc_quantize_channels(1, 2)
+
+        all_tokens = slice(0, N)
+        for tile in range(TILES - 1):
+            for b in range(B):
+                dx_multiply(b, tile, all_tokens, on_scalar)
+            w_interleave(tile + 1, (1, 2))
+            if tile + 2 < TILES:
+                w_interleave(tile + 2, (0,))
+            w_quantize(tile + 1)
+            empty_banks(B)
+        dx_multiply(0, TILES - 1, all_tokens, on_scalar)
+        empty_banks(1)
+        dx_multiply(1, TILES - 1, slice(0, N // 2), on_scalar)
+        dx_multiply(1, TILES - 1, slice(N // 2, N), on_vector)
+        empty_banks(2)

from contextlib import ExitStack

import concourse.mybir as mybir
from concourse.masks import make_identity

F32 = mybir.dt.float32
BF16 = mybir.dt.bfloat16
U32 = mybir.dt.uint32
U8 = mybir.dt.uint8
E4M3 = mybir.dt.float8_e4m3fn_x4
E5M2 = mybir.dt.float8_e5m2_x4
ACT = mybir.ActivationFunctionType
ALU = mybir.AluOpType

P = 128
PACK = 4
B = 2
N = 512
C = 512
GATES = 3
C3 = GATES * C
TILES = C3 // P
Z_TILES = 2 * C // P
BANKS = 8
BOTH = (0, 1)
SIDE_INPUTS = ("grad_0", "m", "grad_1")
RESULT_BUFS = 5
ALIGN = 64

FLOPS = 2 * 2 * C3 * C3 * B * N
BYTES = 2 * B * N * 6 * C + 2 * C3 * C3 + 2 * 4 * B * N * C3 + 4 * C3 * C3


def tile_self_attention_memory_module_pb_v_kernel(
    tc, z, h, m, Wm, bm, combined, grad_0, grad_1, out_0, out_1, out_2
):
    nc = tc.nc
    with ExitStack() as ctx:
        sb = ctx.enter_context(tc.tile_pool(name="sb", bufs=1))
        ps = ctx.enter_context(tc.psum_pool(name="ps", bufs=1))
        ctx.enter_context(tc.manual_schedule())

        free_banks = list(range(BANKS))
        filled = []

        def take_bank():
            number = free_banks[0]
            free_banks.remove(number)
            return number, ps.tile([P, N], F32, name="bank%d" % number)

        def empty_banks(count, skip=0):
            for item in filled[skip : skip + count]:
                filled.remove(item)
                item[1]()
                free_banks.append(item[0])

        ident = sb.tile([P, P], F32, name="ident")
        make_identity(nc, ident[:])

        dc = {}
        for g in range(GATES):
            dc[g] = sb.tile([P, PACK * B * N], BF16, name="dc%d" % g, align_bytes=ALIGN)
        p_tile = sb.tile([P, B * N], F32, name="tmp_p")
        a_tile = sb.tile([P, B * N], F32, name="tmp_a")
        d_tile = sb.tile([P, B * N], F32, name="tmp_d")

        gate_in = {}
        side = {}
        tanh_sq = {}
        x_raw = {}
        w_raw = {}
        staged = {}
        dc_tok = {}
        x_tok = {}
        dc_ch = {}
        w_ch = {}
        results = {}

        def load_combined(j, g, batch=None):
            if (j, g) not in gate_in:
                gate_in[j, g] = sb.tile([P, B * N], F32, name="gate_in", bufs=3 * GATES)
            view = combined.rearrange("b (g p j) y x -> p g j b (y x)", g=GATES, j=PACK)[:, g, j]
            if batch is None:
                nc.sync.dma_start(out=gate_in[j, g][:].rearrange("p (b n) -> p b n", b=B), in_=view)
            else:
                nc.sync.dma_start(out=gate_in[j, g][:, batch * N : (batch + 1) * N], in_=view[:, batch, :])

        sources = {"grad_0": grad_0, "m": m, "grad_1": grad_1}

        def load_side(name, pair, batch=None, member=None):
            if (name, pair) not in side:
                side[name, pair] = sb.tile([P, B * 2 * N], BF16, name="side_%s%d" % (name, pair))
            view = sources[name].rearrange("b (p q j) y x -> p q b j (y x)", q=2, j=2)[:, pair]
            tile = side[name, pair][:].rearrange("p (b j n) -> p b j n", b=B, j=2)
            if batch is None:
                nc.sync.dma_start(out=tile.rearrange("p b j n -> p b (j n)"), in_=view.rearrange("p b j n -> p b (j n)"))
            elif member is None:
                nc.sync.dma_start(out=tile[:, batch], in_=view[:, batch])
            else:
                nc.sync.dma_start(out=tile[:, batch, member], in_=view[:, batch, member])

        def raw_tile():
            return sb.tile([P, PACK * C3], BF16, name="raw", bufs=3, align_bytes=256)

        def load_x(b, group):
            src = z[b, group * C : (group + 1) * C] if group < 2 else h[b]
            nc.sync.dma_start(
                out=x_raw[b][:, group * 4 * N : (group + 1) * 4 * N].rearrange("p (q r) -> p q r", q=2),
                in_=src.rearrange("(q p i) y x -> p q (i y x)", q=2, i=2),
            )

        def load_w(g):
            w_raw[g] = raw_tile()
            nc.sync.dma_start(out=w_raw[g][:], in_=Wm[g * C : (g + 1) * C, :].rearrange("(p j) c -> p (j c)", j=PACK))

        def columns(batches):
            return slice(batches[0] * N, (batches[-1] + 1) * N)

        def activate(j, batches, part):
            cols = columns(batches)
            if part < GATES:
                func = (ACT.Sigmoid, ACT.Tanh, ACT.Sigmoid)[part]
                nc.scalar.activation(out=gate_in[j, part][:, cols], in_=gate_in[j, part][:, cols], func=func)
            else:
                if j not in tanh_sq:
                    tanh_sq[j] = sb.tile([P, B * N], F32, name="tanh_sq", bufs=2)
                nc.scalar.activation(out=tanh_sq[j][:, cols], in_=gate_in[j, 1][:, cols], func=ACT.Square)

        def activations(j, batches):
            for part in range(GATES + 1):
                activate(j, batches, part)

        def step_ops(j, batches):
            cols = columns(batches)
            rows = slice(batches[0], batches[-1] + 1)

            def by_batch(ap):
                return ap.rearrange("p (b n) -> p b n", n=N)

            def side_view(name):
                return side[name, j // 2][:].rearrange("p (b q n) -> p q b n", b=B, q=2)[:, j % 2, rows, :]

            so, t, g = [by_batch(gate_in[j, i][:, cols]) for i in range(GATES)]
            tt = by_batch(tanh_sq[j][:, cols])
            p = by_batch(p_tile[:, cols])
            a = by_batch(a_tile[:, cols])
            d = by_batch(d_tile[:, cols])
            dmo, dmg, dmi = [by_batch(dc[i][:, j * B * N : (j + 1) * B * N][:, cols]) for i in range(GATES)]

            def two(out, in0, in1, op):
                return lambda: nc.vector.tensor_tensor(out=out, in0=in0, in1=in1, op=op)

            def scaled(out, in0, scalar, op0, in1):
                return lambda: nc.vector.scalar_tensor_tensor(
                    out=out, in0=in0, scalar=scalar, in1=in1, op0=op0, op1=ALU.mult
                )

            return [
                two(p, so, side_view("grad_0"), ALU.mult),
                two(a, t, side_view("m"), ALU.subtract),
                scaled(so, so, 1.0, ALU.subtract, p),
                scaled(a, g, 1.0, ALU.subtract, a),
                two(d, p, side_view("grad_1"), ALU.add),
                two(t, t, a, ALU.add),
                scaled(d, d, -1.0, ALU.mult, g),
                scaled(dmo, so, -1.0, ALU.mult, t),
                scaled(dmg, tt, 1.0, ALU.subtract, d),
                two(dmi, d, a, ALU.mult),
            ]

        def transpose_words(bank, place, words):
            for u in range(2):
                col = (2 * place + u) * P
                nc.tensor.transpose(bank[:, col : col + P], words[:, u : 2 * P : 2], ident[:])

        dc_banks = {}

        def dc_transpose(j, g, batches):
            if batches[0] == 0:
                dc_banks[j, g] = take_bank()
            number, bank = dc_banks[j, g]
            for b in batches:
                col = (j * B + b) * N
                transpose_words(bank, b, dc[g][:, col : col + N].bitcast(F32))

            def copy_out():
                staged["dc_tok", j, g] = sb.tile([P, B * N], BF16, name="stage_dc_tok", bufs=GATES, align_bytes=ALIGN)
                nc.scalar.copy(
                    out=staged["dc_tok", j, g][:].bitcast(F32).rearrange("p (s m u) -> p s m u", s=B, u=2),
                    in_=bank[:].rearrange("p (s u m) -> p s m u", s=B, u=2),
                )

            if batches[-1] == B - 1:
                filled.append((number, copy_out))

        def dc_quantize_tokens(j, g):
            codes = sb.tile([P, B * P], U32, name="dc_tok_codes", bufs=GATES, align_bytes=ALIGN)
            scales = sb.tile([P, B * P], U8, name="dc_tok_scales", bufs=GATES, align_bytes=ALIGN)
            dc_tok[j, g] = (codes, scales)
            nc.vector.quantize_mx(out=codes[:].bitcast(E5M2), scales=scales[:], in_=staged["dc_tok", j, g][:])

        def wide_stage():
            return sb.tile([P, PACK * N], BF16, name="stage_wide", bufs=3, align_bytes=ALIGN)

        def x_transpose_half(b, group, q):
            number, bank = take_bank()
            for i in range(2):
                col = (group * 4 + q * 2 + i) * N
                transpose_words(bank, i, x_raw[b][:, col : col + N].bitcast(F32))

            def copy_out():
                if q == 0:
                    staged["x", b, group] = wide_stage()
                half = staged["x", b, group][:, q * 2 * N : (q + 1) * 2 * N]
                nc.scalar.copy(
                    out=half.bitcast(F32).rearrange("p (m i u) -> p m i u", i=2, u=2),
                    in_=bank[:].rearrange("p (i u m) -> p m i u", i=2, u=2),
                )

            filled.append((number, copy_out))

        def x_transpose(group):
            for b in range(B):
                for q in range(2):
                    x_transpose_half(b, group, q)

        def x_quantize(b, group):
            codes = sb.tile([P, C], U32, name="x_codes%d%d" % (b, group), align_bytes=ALIGN)
            scales = sb.tile([P, C], U8, name="x_scales%d%d" % (b, group), align_bytes=ALIGN)
            x_tok[b, group] = (codes, scales)
            nc.vector.quantize_mx(out=codes[:].bitcast(E4M3), scales=scales[:], in_=staged["x", b, group][:])

        dw_view = out_2.rearrange("(g p j) c -> p g j c", g=GATES, j=PACK)

        def result_tile():
            return sb.tile([P, GATES * N], F32, name="result", bufs=RESULT_BUFS)

        def dw_multiply(j, g, group):
            number, bank = take_bank()
            for b in range(B):
                cols = slice(b * P, (b + 1) * P)
                nc.tensor.matmul_mx(
                    out=bank[:],
                    lhsT=dc_tok[j, g][0][:, cols].bitcast(E5M2),
                    lhsT_scale=dc_tok[j, g][1][:, cols],
                    rhs=x_tok[b, group][0][:].bitcast(E4M3),
                    rhs_scale=x_tok[b, group][1][:],
                    start=(b == 0),
                    stop=(b == B - 1),
                )

            def copy_out():
                place = g if j == 0 else group
                if place == 0:
                    results["dw"] = result_tile()
                res = results["dw"]
                nc.scalar.copy(out=res[:, place * N : (place + 1) * N], in_=bank[:])
                if place == GATES - 1 and j == 0:
                    nc.sync.dma_start(
                        out=dw_view[:, :, j, group * C : (group + 1) * C],
                        in_=res[:].rearrange("p (g n) -> p g n", g=GATES),
                    )
                elif place == GATES - 1:
                    nc.sync.dma_start(out=dw_view[:, g, j, :], in_=res[:])

            filled.append((number, copy_out))

        def dw_first_rows(group):
            for g in range(GATES):
                dw_multiply(0, g, group)

        def dw_rows(j):
            for g in range(GATES):
                for group in range(GATES):
                    dw_multiply(j, g, group)
                empty_banks(GATES)

        def interleave(copy, dst, src):
            copy(
                out=dst.rearrange("p (c i j) -> p c j i", i=4, j=PACK),
                in_=src.rearrange("p j (c i) -> p c j i", i=4),
            )

        def dc_interleave(b, g, copy):
            staged["dc_ch", b, g] = wide_stage()
            rows = dc[g][:].rearrange("p (j b n) -> p b j n", j=PACK, b=B)[:, b]
            interleave(copy, staged["dc_ch", b, g][:], rows)

        def dc_quantize_channels(b, g):
            codes = sb.tile([P, N], U32, name="dc_ch_codes%d%d" % (b, g), align_bytes=ALIGN)
            scales = sb.tile([P, N], U8, name="dc_ch_scales%d%d" % (b, g), align_bytes=ALIGN)
            dc_ch[b, g] = (codes, scales)
            nc.vector.quantize_mx(out=codes[:].bitcast(E5M2), scales=scales[:], in_=staged["dc_ch", b, g][:])

        def w_interleave(tile, gates):
            if gates[0] == 0:
                staged["w", tile] = sb.tile([P, GATES * PACK * P], BF16, name="stage_w", bufs=3, align_bytes=ALIGN)
            for g in gates:
                rows = w_raw[g][:].rearrange("p (j c) -> p j c", j=PACK)
                interleave(
                    nc.vector.tensor_copy,
                    staged["w", tile][:, g * PACK * P : (g + 1) * PACK * P],
                    rows[:, :, tile * P : (tile + 1) * P],
                )

        def w_quantize(tile):
            codes = sb.tile([P, GATES * P], U32, name="w_codes", bufs=3, align_bytes=ALIGN)
            scales = sb.tile([P, GATES * P], U8, name="w_scales", bufs=3, align_bytes=ALIGN)
            nc.vector.quantize_mx(out=codes[:].bitcast(E4M3), scales=scales[:], in_=staged["w", tile][:])
            for g in range(GATES):
                cols = slice(g * P, (g + 1) * P)
                w_ch[tile, g] = (codes[:, cols], scales[:, cols])

        def dx_multiply(b, tile, tokens, copy):
            number, bank = take_bank()
            width = tokens.stop - tokens.start
            for g in range(GATES):
                nc.tensor.matmul_mx(
                    out=bank[:, 0:width],
                    lhsT=w_ch[tile, g][0].bitcast(E4M3),
                    lhsT_scale=w_ch[tile, g][1],
                    rhs=dc_ch[b, g][0][:, tokens].bitcast(E5M2),
                    rhs_scale=dc_ch[b, g][1][:, tokens],
                    start=(g == 0),
                    stop=(g == GATES - 1),
                )

            def copy_out():
                if tile < Z_TILES:
                    rows = out_0[:, tile * P : (tile + 1) * P]
                else:
                    rows = out_1[:, (tile - Z_TILES) * P : (tile - Z_TILES + 1) * P]
                dst = rows.rearrange("b p y x -> p b (y x)")
                if b == 0:
                    results["dx"] = result_tile()
                res = results["dx"][:, 0 : B * N].rearrange("p (b n) -> p b n", b=B)
                copy(out=res[:, b, tokens], in_=bank[:, 0:width])
                if tile >= TILES - 2:
                    nc.sync.dma_start(out=dst[:, b, tokens], in_=res[:, b, tokens])
                elif b == B - 1:
                    nc.sync.dma_start(out=dst, in_=res)

            filled.append((number, copy_out))

        on_vector = nc.vector.tensor_copy
        on_scalar = nc.scalar.copy

        def run(ops):
            for op in ops:
                op()

        for b in range(B):
            x_raw[b] = raw_tile()
        for g, name in enumerate(SIDE_INPUTS):
            load_combined(0, g, 0)
            load_side(name, 0, 0, 0)
        for b in range(B):
            load_x(b, 0)
        for g, name in enumerate(SIDE_INPUTS):
            load_combined(0, g, 1)
            load_side(name, 0, 1)
        for g, name in enumerate(SIDE_INPUTS):
            load_combined(1, g)
            load_side(name, 0, 0, 1)
        for group in range(1, GATES):
            for b in range(B):
                load_x(b, group)
        for g, name in enumerate(SIDE_INPUTS):
            load_combined(2, g)
            load_side(name, 1)

        activations(0, (0,))
        x_transpose(0)
        for part in range(GATES + 1):
            empty_banks(1)
            activate(0, (1,), part)
        run(step_ops(0, (0,)))
        for g in range(GATES):
            dc_transpose(0, g, (0,))
        activations(1, BOTH)
        run(step_ops(0, (1,)))
        for g in range(GATES):
            load_combined(3, g)

        ops = step_ops(1, BOTH)
        for g in range(GATES):
            dc_transpose(0, g, (1,))
        x_transpose(1)
        empty_banks(GATES)
        for b in range(B):
            ops[b]()
            x_quantize(b, 0)
        ops[2]()
        for g in range(GATES):
            dc_quantize_tokens(0, g)
        dw_first_rows(0)
        empty_banks(2 * B)
        x_transpose(2)
        ops[3]()
        for b in range(B):
            ops[4 + b]()
            x_quantize(b, 1)
        activate(2, BOTH, 0)
        empty_banks(GATES)
        load_w(0)
        dw_first_rows(1)
        activate(2, BOTH, 1)
        empty_banks(2 * B)
        activate(2, BOTH, 2)
        ops[6]()
        for b in range(B):
            ops[7 + b]()
            x_quantize(b, 2)
        dw_first_rows(2)
        ops[9]()
        empty_banks(GATES)
        load_w(1)
        activate(2, BOTH, 3)

        ops = step_ops(2, BOTH)
        for g in range(GATES):
            dc_transpose(1, g, BOTH)
        empty_banks(GATES, skip=GATES)
        empty_banks(GATES)
        load_w(2)
        run(ops[:2])
        activations(3, (0,))
        for g in range(GATES):
            ops[2 + g]()
            dc_quantize_tokens(1, g)
        dw_rows(1)
        run(ops[5:7])
        for g in range(GATES):
            ops[7 + g]()
            dc_transpose(2, g, BOTH)

        ops = step_ops(3, (0,))
        empty_banks(GATES)
        activations(3, (1,))
        run(ops[:2])
        for g in range(GATES):
            ops[2 + g]()
            dc_quantize_tokens(2, g)
        dw_rows(2)
        run(ops[5:])

        ops = step_ops(3, (1,))
        for g in range(GATES):
            dc_transpose(3, g, (0,))
        dc_interleave(0, 0, on_scalar)
        run(ops[:7])
        for g in range(GATES):
            ops[7 + g]()
            dc_transpose(3, g, (1,))
        empty_banks(GATES)

        dc_quantize_channels(0, 0)
        dc_interleave(0, 1, on_vector)
        dc_quantize_tokens(3, 0)
        dc_interleave(1, 0, on_vector)
        dc_quantize_channels(0, 1)
        dc_interleave(0, 2, on_scalar)
        dc_quantize_tokens(3, 1)
        dc_quantize_tokens(3, 2)
        dc_quantize_channels(1, 0)
        dc_interleave(1, 2, on_scalar)
        dw_rows(3)
        w_interleave(0, range(GATES))
        dc_quantize_channels(0, 2)
        w_quantize(0)
        dc_interleave(1, 1, on_vector)
        w_interleave(1, (0,))
        dc_quantize_channels(1, 1)
        dc_quantize_channels(1, 2)

        all_tokens = slice(0, N)
        for tile in range(TILES - 1):
            for b in range(B):
                dx_multiply(b, tile, all_tokens, on_scalar)
            w_interleave(tile + 1, (1, 2))
            if tile + 2 < TILES:
                w_interleave(tile + 2, (0,))
            w_quantize(tile + 1)
            empty_banks(B)
        dx_multiply(0, TILES - 1, all_tokens, on_scalar)
        empty_banks(1)
        dx_multiply(1, TILES - 1, slice(0, N // 2), on_scalar)
        dx_multiply(1, TILES - 1, slice(N // 2, N), on_vector)
        empty_banks(2)
